import numpy as np
import ml_dtypes


def mxq(x, axis, fmt="e4m3"):
    dtype, down = {"e4m3": (ml_dtypes.float8_e4m3fn, 7), "e5m2": (ml_dtypes.float8_e5m2, 14)}[fmt]
    v = np.moveaxis(np.asarray(x, np.float32).astype(ml_dtypes.bfloat16).astype(np.float64), axis, -1)
    blocks = v.reshape(v.shape[:-1] + (-1, 32))
    amax = np.abs(blocks).max(-1, keepdims=True)
    byte = np.maximum(np.where(amax > 0, np.frexp(amax)[1] - 1 + 127, 0) - down, 1)
    scale = np.exp2(byte - 127.0)
    codes = (blocks / scale).astype(np.float32).astype(dtype).astype(np.float64)
    return np.moveaxis((codes * scale).reshape(v.shape), -1, axis)


WIDE = False


def mx_kscale(k):
    if not WIDE:
        return np.ones(k)
    levels = np.array([20, -20, 10, -10, 0])
    a = np.random.permutation(np.resize(levels, k // 512 * 4)).reshape(k // 512, 4)
    idx = np.arange(k)
    return np.exp2(a[idx // 512, idx % 128 // 32])


BF16 = ml_dtypes.bfloat16


def bf(x):
    return np.asarray(x, np.float32).astype(BF16)


def f64(x):
    return np.asarray(x).astype(np.float64)


T, B, I, H = 12, 128, 512, 1024


def sigmoid(v):
    return 1.0 / (1.0 + np.exp(-v))


def setup_inputs():
    s = mx_kscale(T * B).reshape(T, B)
    x0 = bf(np.random.standard_normal((T, B, I)))
    W_ih = bf(np.random.standard_normal((3 * H, I)) / np.sqrt(I))
    b_ih = bf(np.random.standard_normal(3 * H) * 0.3)
    gh = bf(np.random.standard_normal((B, 3 * H)) * 0.5)
    g = bf(np.random.standard_normal((B, T, H)) * np.exp2(np.random.randint(-12, 1, (B, T, 1))) * 4.0
           / np.transpose(s)[:, :, None])
    gi = f64(x0) @ f64(W_ih).T + f64(b_ih)
    gg = f64(gh)
    r = sigmoid(gi[..., :H] + gg[..., :H])
    z = sigmoid(gi[..., H:2 * H] + gg[..., H:2 * H])
    n = np.tanh(gi[..., 2 * H:] + r * gg[..., 2 * H:])
    return {"input_seq": bf(f64(x0) * s[:, :, None]), "W_ih": W_ih, "b_ih": b_ih, "gh": gh,
            "r": np.asarray(r, np.float32), "z": np.asarray(z, np.float32), "n": np.asarray(n, np.float32),
            "grad_out": g}


def reference(input_seq, W_ih, b_ih, gh, r, z, n, grad_out):
    rf, zf, nf = f64(r), f64(z), f64(n)
    h_n = f64(gh)[:, 2 * H:]
    dh = np.transpose(f64(grad_out), (1, 0, 2))
    d_n = dh * (1.0 - zf) * (1.0 - nf * nf)
    d_z = -dh * nf * zf * (1.0 - zf)
    d_r = d_n * h_n * rf * (1.0 - rf)
    dgi = np.concatenate([d_r, d_z, d_n], axis=2).reshape(T * B, 3 * H)
    xs = f64(input_seq).reshape(T * B, I)
    return mxq(dgi, 0, "e5m2").T @ mxq(xs, 0, "e4m3")

@@ -1,0 +1,153 @@
+from contextlib import ExitStack
+
+import concourse.mybir as mybir
+
+F32 = mybir.dt.float32
+BF16 = mybir.dt.bfloat16
+U32 = mybir.dt.uint32
+U8 = mybir.dt.uint8
+E4M3_X4 = mybir.dt.float8_e4m3fn_x4
+E5M2_X4 = mybir.dt.float8_e5m2_x4
+ALU = mybir.AluOpType
+ACT = mybir.ActivationFunctionType
+
+T, B, I, H = 12, 128, 512, 1024
+P = 128
+PACK = 4
+PASSES = T // PACK
+GATES = 3
+M_TILE = 128
+H_ROUND = 256
+ROUNDS = H // H_ROUND
+HALVES = H_ROUND // M_TILE
+
+FLOPS = 2 * T * B * GATES * H * I
+BYTES = T * B * I * 2 + B * H * 2 + 3 * T * B * H * 4 + B * T * H * 2 + GATES * H * I * 4
+
+
+def rows_in_fours(rows):
+    return rows.rearrange("p j (c i) -> p c j i", i=4)
+
+
+def words_in_fours(words):
+    return words.rearrange("p (c i) j -> p c j i", i=4)
+
+
+def tile_grucellmodel_pa_v_kernel(tc, input_seq, W_ih, b_ih, gh, r, z, n, grad_out, out):
+    nc = tc.nc
+    with ExitStack() as ctx:
+        keep = ctx.enter_context(tc.tile_pool(name="keep", bufs=1))
+        loads = ctx.enter_context(tc.tile_pool(name="loads", bufs=3))
+        work = ctx.enter_context(tc.tile_pool(name="work", bufs=2))
+        grouped = ctx.enter_context(tc.tile_pool(name="grouped", bufs=2))
+        packed = ctx.enter_context(tc.tile_pool(name="packed", bufs=2))
+        results = ctx.enter_context(tc.tile_pool(name="results", bufs=4))
+        psum = ctx.enter_context(tc.psum_pool(name="psum", bufs=8))
+
+        h_n = keep.tile([P, H], BF16)
+        minus_h_n = keep.tile([P, H], BF16)
+        x_rows = keep.tile([P, PASSES, PACK, I], BF16)
+        x_codes = keep.tile([P, PASSES, I], U32, align_bytes=64)
+        x_scales = keep.tile([P, PASSES, I], U8, align_bytes=64)
+
+        for hq in range(ROUNDS):
+            h_cols = slice(hq * H_ROUND, (hq + 1) * H_ROUND)
+            acc = [
+                [psum.tile([M_TILE, I], F32, name="acc", tag="acc") for half in range(HALVES)]
+                for gate in range(GATES)
+            ]
+            for c in range(PASSES):
+                steps = slice(c * PACK, (c + 1) * PACK)
+
+                z_t = loads.tile([P, PACK, H_ROUND], F32)
+                nc.sync.dma_start(out=z_t[:], in_=z[steps, :, h_cols].rearrange("j b h -> b j h"))
+                g_t = loads.tile([P, PACK, H_ROUND], BF16)
+                nc.sync.dma_start(out=g_t[:], in_=grad_out[:, steps, h_cols])
+                n_t = loads.tile([P, PACK, H_ROUND], F32)
+                nc.sync.dma_start(out=n_t[:], in_=n[steps, :, h_cols].rearrange("j b h -> b j h"))
+                r_t = loads.tile([P, PACK, H_ROUND], F32)
+                nc.sync.dma_start(out=r_t[:], in_=r[steps, :, h_cols].rearrange("j b h -> b j h"))
+
+                if hq == 0 and c == 0:
+                    nc.sync.dma_start(out=h_n[:], in_=gh[:, 2 * H : 3 * H])
+                    nc.scalar.mul(out=minus_h_n[:], in_=h_n[:], mul=-1.0)
+
+                if hq == 0:
+                    nc.sync.dma_start(
+                        out=x_rows[:, c, :, :], in_=input_seq[steps].rearrange("j b i -> b j i")
+                    )
+                    x_words = grouped.tile([P, I, PACK], BF16, align_bytes=64)
+                    nc.scalar.copy(out=words_in_fours(x_words[:]), in_=rows_in_fours(x_rows[:, c, :, :]))
+                    nc.vector.quantize_mx(
+                        out=x_codes[:, c, :].bitcast(E4M3_X4),
+                        scales=x_scales[:, c, :],
+                        in_=x_words[:].rearrange("p w j -> p (w j)"),
+                    )
+
+                w = work.tile([P, PACK, H_ROUND], F32)
+                nc.vector.scalar_tensor_tensor(
+                    out=w[:], in0=z_t[:], scalar=1.0, in1=g_t[:], op0=ALU.subtract, op1=ALU.mult
+                )
+                nz = work.tile([P, PACK, H_ROUND], F32)
+                nc.vector.tensor_tensor(out=nz[:], in0=n_t[:], in1=z_t[:], op=ALU.mult)
+                rr = work.tile([P, PACK, H_ROUND], F32)
+                nc.vector.scalar_tensor_tensor(
+                    out=rr[:], in0=r_t[:], scalar=1.0, in1=r_t[:], op0=ALU.subtract, op1=ALU.mult
+                )
+                nn = work.tile([P, PACK, H_ROUND], F32)
+                nc.scalar.activation(out=nn[:], in_=n_t[:], func=ACT.Square)
+                d_n = work.tile([P, PACK, H_ROUND], F32)
+                nc.vector.scalar_tensor_tensor(
+                    out=d_n[:], in0=nn[:], scalar=1.0, in1=w[:], op0=ALU.subtract, op1=ALU.mult
+                )
+                rh = work.tile([P, PACK, H_ROUND], F32)
+                nc.vector.tensor_tensor(
+                    out=rh[:],
+                    in0=rr[:],
+                    in1=minus_h_n[:, h_cols].unsqueeze(1).to_broadcast([P, PACK, H_ROUND]),
+                    op=ALU.mult,
+                )
+
+                dz_words = grouped.tile([P, H_ROUND, PACK], BF16, align_bytes=64)
+                nc.vector.tensor_tensor(
+                    out=words_in_fours(dz_words[:]),
+                    in0=rows_in_fours(w[:]),
+                    in1=rows_in_fours(nz[:]),
+                    op=ALU.mult,
+                )
+                dn_words = grouped.tile([P, H_ROUND, PACK], BF16, align_bytes=64)
+                nc.scalar.copy(out=words_in_fours(dn_words[:]), in_=rows_in_fours(d_n[:]))
+                dr_words = grouped.tile([P, H_ROUND, PACK], BF16, align_bytes=64)
+                nc.vector.tensor_tensor(
+                    out=words_in_fours(dr_words[:]),
+                    in0=rows_in_fours(rh[:]),
+                    in1=rows_in_fours(d_n[:]),
+                    op=ALU.mult,
+                )
+
+                codes = packed.tile([P, GATES, H_ROUND], U32, align_bytes=64)
+                scales = packed.tile([P, GATES, H_ROUND], U8, align_bytes=64)
+                for gate, words in ((1, dz_words), (2, dn_words), (0, dr_words)):
+                    nc.vector.quantize_mx(
+                        out=codes[:, gate, :].bitcast(E5M2_X4),
+                        scales=scales[:, gate, :],
+                        in_=words[:].rearrange("p w j -> p (w j)"),
+                    )
+                    for half in range(HALVES):
+                        m_cols = slice(half * M_TILE, (half + 1) * M_TILE)
+                        nc.tensor.matmul_mx(
+                            out=acc[gate][half][:],
+                            lhsT=codes[:, gate, m_cols].bitcast(E5M2_X4),
+                            lhsT_scale=scales[:, gate, m_cols],
+                            rhs=x_codes[:, c, :].bitcast(E4M3_X4),
+                            rhs_scale=x_scales[:, c, :],
+                            start=(c == 0),
+                            stop=(c == PASSES - 1),
+                        )
+
+            for gate in range(GATES):
+                for half in range(HALVES):
+                    row0 = gate * H + hq * H_ROUND + half * M_TILE
+                    res = results.tile([M_TILE, I], F32)
+                    nc.scalar.copy(out=res[:], in_=acc[gate][half][:])
+                    nc.scalar.dma_start(out=out[row0 : row0 + M_TILE, :], in_=res[:])

@@ -20,6 +20,7 @@ M_TILE = 128
 H_ROUND = 256
 ROUNDS = H // H_ROUND
 HALVES = H_ROUND // M_TILE
+GATE_ORDER = (1, 2, 0)
 
 FLOPS = 2 * T * B * GATES * H * I
 BYTES = T * B * I * 2 + B * H * 2 + 3 * T * B * H * 4 + B * T * H * 2 + GATES * H * I * 4
@@ -37,7 +38,7 @@ def tile_grucellmodel_pa_v_kernel(tc, input_seq, W_ih, b_ih, gh, r, z, n, grad_o
     nc = tc.nc
     with ExitStack() as ctx:
         keep = ctx.enter_context(tc.tile_pool(name="keep", bufs=1))
-        loads = ctx.enter_context(tc.tile_pool(name="loads", bufs=3))
+        loads = ctx.enter_context(tc.tile_pool(name="loads", bufs=4))
         work = ctx.enter_context(tc.tile_pool(name="work", bufs=2))
         grouped = ctx.enter_context(tc.tile_pool(name="grouped", bufs=2))
         packed = ctx.enter_context(tc.tile_pool(name="packed", bufs=2))
@@ -46,6 +47,8 @@ def tile_grucellmodel_pa_v_kernel(tc, input_seq, W_ih, b_ih, gh, r, z, n, grad_o
 
         h_n = keep.tile([P, H], BF16)
         minus_h_n = keep.tile([P, H], BF16)
+        minus_half = keep.tile([P, 1], F32)
+        nc.vector.memset(minus_half[:], -0.5)
         x_rows = keep.tile([P, PASSES, PACK, I], BF16)
         x_codes = keep.tile([P, PASSES, I], U32, align_bytes=64)
         x_scales = keep.tile([P, PASSES, I], U8, align_bytes=64)
@@ -90,10 +93,8 @@ def tile_grucellmodel_pa_v_kernel(tc, input_seq, W_ih, b_ih, gh, r, z, n, grad_o
                 )
                 nz = work.tile([P, PACK, H_ROUND], F32)
                 nc.vector.tensor_tensor(out=nz[:], in0=n_t[:], in1=z_t[:], op=ALU.mult)
-                rr = work.tile([P, PACK, H_ROUND], F32)
-                nc.vector.scalar_tensor_tensor(
-                    out=rr[:], in0=r_t[:], scalar=1.0, in1=r_t[:], op0=ALU.subtract, op1=ALU.mult
-                )
+                rc2 = work.tile([P, PACK, H_ROUND], F32)
+                nc.scalar.activation(out=rc2[:], in_=r_t[:], func=ACT.Square, bias=minus_half[:])
                 nn = work.tile([P, PACK, H_ROUND], F32)
                 nc.scalar.activation(out=nn[:], in_=n_t[:], func=ACT.Square)
                 d_n = work.tile([P, PACK, H_ROUND], F32)
@@ -101,11 +102,13 @@ def tile_grucellmodel_pa_v_kernel(tc, input_seq, W_ih, b_ih, gh, r, z, n, grad_o
                     out=d_n[:], in0=nn[:], scalar=1.0, in1=w[:], op0=ALU.subtract, op1=ALU.mult
                 )
                 rh = work.tile([P, PACK, H_ROUND], F32)
-                nc.vector.tensor_tensor(
+                nc.vector.scalar_tensor_tensor(
                     out=rh[:],
-                    in0=rr[:],
+                    in0=rc2[:],
+                    scalar=0.25,
                     in1=minus_h_n[:, h_cols].unsqueeze(1).to_broadcast([P, PACK, H_ROUND]),
-                    op=ALU.mult,
+                    op0=ALU.subtract,
+                    op1=ALU.mult,
                 )
 
                 dz_words = grouped.tile([P, H_ROUND, PACK], BF16, align_bytes=64)
@@ -127,7 +130,9 @@ def tile_grucellmodel_pa_v_kernel(tc, input_seq, W_ih, b_ih, gh, r, z, n, grad_o
 
                 codes = packed.tile([P, GATES, H_ROUND], U32, align_bytes=64)
                 scales = packed.tile([P, GATES, H_ROUND], U8, align_bytes=64)
-                for gate, words in ((1, dz_words), (2, dn_words), (0, dr_words)):
+                words_of = {0: dr_words, 1: dz_words, 2: dn_words}
+                for gate in GATE_ORDER:
+                    words = words_of[gate]
                     nc.vector.quantize_mx(
                         out=codes[:, gate, :].bitcast(E5M2_X4),
                         scales=scales[:, gate, :],
@@ -145,9 +150,13 @@ def tile_grucellmodel_pa_v_kernel(tc, input_seq, W_ih, b_ih, gh, r, z, n, grad_o
                             stop=(c == PASSES - 1),
                         )
 
-            for gate in range(GATES):
+            for gate in GATE_ORDER:
                 for half in range(HALVES):
                     row0 = gate * H + hq * H_ROUND + half * M_TILE
                     res = results.tile([M_TILE, I], F32)
-                    nc.scalar.copy(out=res[:], in_=acc[gate][half][:])
-                    nc.scalar.dma_start(out=out[row0 : row0 + M_TILE, :], in_=res[:])
+                    if hq == ROUNDS - 1 and gate == GATE_ORDER[-1] and half == HALVES - 1:
+                        nc.vector.tensor_copy(out=res[:], in_=acc[gate][half][:])
+                        nc.sync.dma_start(out=out[row0 : row0 + M_TILE, :], in_=res[:])
+                    else:
+                        nc.scalar.copy(out=res[:], in_=acc[gate][half][:])
+                        nc.scalar.dma_start(out=out[row0 : row0 + M_TILE, :], in_=res[:])

@@ -16,11 +16,14 @@ P = 128
 PACK = 4
 PASSES = T // PACK
 GATES = 3
+GATE_ORDER = (1, 2, 0)
 M_TILE = 128
 H_ROUND = 256
 ROUNDS = H // H_ROUND
 HALVES = H_ROUND // M_TILE
-GATE_ORDER = (1, 2, 0)
+STEPS = ROUNDS * PASSES
+LOADS_AHEAD = 3
+SQUARES_AHEAD = 2
 
 FLOPS = 2 * T * B * GATES * H * I
 BYTES = T * B * I * 2 + B * H * 2 + 3 * T * B * H * 4 + B * T * H * 2 + GATES * H * I * 4
@@ -38,125 +41,153 @@ def tile_grucellmodel_pa_v_kernel(tc, input_seq, W_ih, b_ih, gh, r, z, n, grad_o
     nc = tc.nc
     with ExitStack() as ctx:
         keep = ctx.enter_context(tc.tile_pool(name="keep", bufs=1))
-        loads = ctx.enter_context(tc.tile_pool(name="loads", bufs=4))
+        loads = ctx.enter_context(tc.tile_pool(name="loads", bufs=LOADS_AHEAD + 1))
+        ahead = ctx.enter_context(tc.tile_pool(name="ahead", bufs=SQUARES_AHEAD + 1))
         work = ctx.enter_context(tc.tile_pool(name="work", bufs=2))
         grouped = ctx.enter_context(tc.tile_pool(name="grouped", bufs=2))
         packed = ctx.enter_context(tc.tile_pool(name="packed", bufs=2))
-        results = ctx.enter_context(tc.tile_pool(name="results", bufs=4))
+        results = ctx.enter_context(tc.tile_pool(name="results", bufs=GATES * HALVES))
         psum = ctx.enter_context(tc.psum_pool(name="psum", bufs=8))
+        ctx.enter_context(tc.manual_schedule())
 
         h_n = keep.tile([P, H], BF16)
         minus_h_n = keep.tile([P, H], BF16)
         minus_half = keep.tile([P, 1], F32)
-        nc.vector.memset(minus_half[:], -0.5)
         x_rows = keep.tile([P, PASSES, PACK, I], BF16)
         x_codes = keep.tile([P, PASSES, I], U32, align_bytes=64)
         x_scales = keep.tile([P, PASSES, I], U8, align_bytes=64)
+        loaded = {}
+        squared = {}
+        x_grouped = {}
 
-        for hq in range(ROUNDS):
+        def load(s):
+            hq, c = divmod(s, PASSES)
+            steps = slice(c * PACK, (c + 1) * PACK)
             h_cols = slice(hq * H_ROUND, (hq + 1) * H_ROUND)
-            acc = [
-                [psum.tile([M_TILE, I], F32, name="acc", tag="acc") for half in range(HALVES)]
-                for gate in range(GATES)
-            ]
-            for c in range(PASSES):
-                steps = slice(c * PACK, (c + 1) * PACK)
-
-                z_t = loads.tile([P, PACK, H_ROUND], F32)
-                nc.sync.dma_start(out=z_t[:], in_=z[steps, :, h_cols].rearrange("j b h -> b j h"))
-                g_t = loads.tile([P, PACK, H_ROUND], BF16)
-                nc.sync.dma_start(out=g_t[:], in_=grad_out[:, steps, h_cols])
-                n_t = loads.tile([P, PACK, H_ROUND], F32)
-                nc.sync.dma_start(out=n_t[:], in_=n[steps, :, h_cols].rearrange("j b h -> b j h"))
-                r_t = loads.tile([P, PACK, H_ROUND], F32)
-                nc.sync.dma_start(out=r_t[:], in_=r[steps, :, h_cols].rearrange("j b h -> b j h"))
-
-                if hq == 0 and c == 0:
-                    nc.sync.dma_start(out=h_n[:], in_=gh[:, 2 * H : 3 * H])
-                    nc.scalar.mul(out=minus_h_n[:], in_=h_n[:], mul=-1.0)
-
-                if hq == 0:
-                    nc.sync.dma_start(
-                        out=x_rows[:, c, :, :], in_=input_seq[steps].rearrange("j b i -> b j i")
-                    )
-                    x_words = grouped.tile([P, I, PACK], BF16, align_bytes=64)
-                    nc.scalar.copy(out=words_in_fours(x_words[:]), in_=rows_in_fours(x_rows[:, c, :, :]))
-                    nc.vector.quantize_mx(
-                        out=x_codes[:, c, :].bitcast(E4M3_X4),
-                        scales=x_scales[:, c, :],
-                        in_=x_words[:].rearrange("p w j -> p (w j)"),
-                    )
-
-                w = work.tile([P, PACK, H_ROUND], F32)
-                nc.vector.scalar_tensor_tensor(
-                    out=w[:], in0=z_t[:], scalar=1.0, in1=g_t[:], op0=ALU.subtract, op1=ALU.mult
-                )
-                nz = work.tile([P, PACK, H_ROUND], F32)
-                nc.vector.tensor_tensor(out=nz[:], in0=n_t[:], in1=z_t[:], op=ALU.mult)
-                rc2 = work.tile([P, PACK, H_ROUND], F32)
-                nc.scalar.activation(out=rc2[:], in_=r_t[:], func=ACT.Square, bias=minus_half[:])
-                nn = work.tile([P, PACK, H_ROUND], F32)
-                nc.scalar.activation(out=nn[:], in_=n_t[:], func=ACT.Square)
-                d_n = work.tile([P, PACK, H_ROUND], F32)
-                nc.vector.scalar_tensor_tensor(
-                    out=d_n[:], in0=nn[:], scalar=1.0, in1=w[:], op0=ALU.subtract, op1=ALU.mult
-                )
-                rh = work.tile([P, PACK, H_ROUND], F32)
-                nc.vector.scalar_tensor_tensor(
-                    out=rh[:],
-                    in0=rc2[:],
-                    scalar=0.25,
-                    in1=minus_h_n[:, h_cols].unsqueeze(1).to_broadcast([P, PACK, H_ROUND]),
-                    op0=ALU.subtract,
-                    op1=ALU.mult,
+            z_t = loads.tile([P, PACK, H_ROUND], F32)
+            nc.sync.dma_start(out=z_t[:], in_=z[steps, :, h_cols].rearrange("j b h -> b j h"))
+            g_t = loads.tile([P, PACK, H_ROUND], BF16)
+            nc.sync.dma_start(out=g_t[:], in_=grad_out[:, steps, h_cols])
+            n_t = loads.tile([P, PACK, H_ROUND], F32)
+            nc.sync.dma_start(out=n_t[:], in_=n[steps, :, h_cols].rearrange("j b h -> b j h"))
+            r_t = loads.tile([P, PACK, H_ROUND], F32)
+            nc.sync.dma_start(out=r_t[:], in_=r[steps, :, h_cols].rearrange("j b h -> b j h"))
+            loaded[s] = (z_t, g_t, n_t, r_t)
+            if s == 0:
+                nc.sync.dma_start(out=h_n[:], in_=gh[:, 2 * H : 3 * H])
+            if hq == 0:
+                nc.sync.dma_start(
+                    out=x_rows[:, c, :, :], in_=input_seq[steps].rearrange("j b i -> b j i")
                 )
 
-                dz_words = grouped.tile([P, H_ROUND, PACK], BF16, align_bytes=64)
-                nc.vector.tensor_tensor(
-                    out=words_in_fours(dz_words[:]),
-                    in0=rows_in_fours(w[:]),
-                    in1=rows_in_fours(nz[:]),
-                    op=ALU.mult,
-                )
-                dn_words = grouped.tile([P, H_ROUND, PACK], BF16, align_bytes=64)
-                nc.scalar.copy(out=words_in_fours(dn_words[:]), in_=rows_in_fours(d_n[:]))
-                dr_words = grouped.tile([P, H_ROUND, PACK], BF16, align_bytes=64)
-                nc.vector.tensor_tensor(
-                    out=words_in_fours(dr_words[:]),
-                    in0=rows_in_fours(rh[:]),
-                    in1=rows_in_fours(d_n[:]),
-                    op=ALU.mult,
-                )
+        def square(s):
+            z_t, g_t, n_t, r_t = loaded[s]
+            nn = ahead.tile([P, PACK, H_ROUND], F32)
+            nc.scalar.activation(out=nn[:], in_=n_t[:], func=ACT.Square)
+            rc2 = ahead.tile([P, PACK, H_ROUND], F32)
+            nc.scalar.activation(out=rc2[:], in_=r_t[:], func=ACT.Square, bias=minus_half[:])
+            squared[s] = (nn, rc2)
 
-                codes = packed.tile([P, GATES, H_ROUND], U32, align_bytes=64)
-                scales = packed.tile([P, GATES, H_ROUND], U8, align_bytes=64)
-                words_of = {0: dr_words, 1: dz_words, 2: dn_words}
-                for gate in GATE_ORDER:
-                    words = words_of[gate]
-                    nc.vector.quantize_mx(
-                        out=codes[:, gate, :].bitcast(E5M2_X4),
-                        scales=scales[:, gate, :],
-                        in_=words[:].rearrange("p w j -> p (w j)"),
-                    )
+        def group_x(c):
+            x_words = grouped.tile([P, I, PACK], BF16, align_bytes=64)
+            nc.scalar.copy(out=words_in_fours(x_words[:]), in_=rows_in_fours(x_rows[:, c, :, :]))
+            x_grouped[c] = x_words
+
+        nc.vector.memset(minus_half[:], -0.5)
+        for s in range(LOADS_AHEAD):
+            load(s)
+        square(0)
+        nc.scalar.mul(out=minus_h_n[:], in_=h_n[:], mul=-1.0)
+        group_x(0)
+        square(1)
+
+        acc = {}
+        for s in range(STEPS):
+            hq, c = divmod(s, PASSES)
+            h_cols = slice(hq * H_ROUND, (hq + 1) * H_ROUND)
+            if s + LOADS_AHEAD < STEPS:
+                load(s + LOADS_AHEAD)
+            z_t, g_t, n_t, r_t = loaded[s]
+            nn, rc2 = squared[s]
+
+            w = work.tile([P, PACK, H_ROUND], F32)
+            nc.vector.scalar_tensor_tensor(
+                out=w[:], in0=z_t[:], scalar=1.0, in1=g_t[:], op0=ALU.subtract, op1=ALU.mult
+            )
+            nz = work.tile([P, PACK, H_ROUND], F32)
+            nc.vector.tensor_tensor(out=nz[:], in0=n_t[:], in1=z_t[:], op=ALU.mult)
+            d_n = work.tile([P, PACK, H_ROUND], F32)
+            nc.vector.scalar_tensor_tensor(
+                out=d_n[:], in0=nn[:], scalar=1.0, in1=w[:], op0=ALU.subtract, op1=ALU.mult
+            )
+            dn_words = grouped.tile([P, H_ROUND, PACK], BF16, align_bytes=64)
+            nc.scalar.copy(out=words_in_fours(dn_words[:]), in_=rows_in_fours(d_n[:]))
+            if s + SQUARES_AHEAD < STEPS:
+                square(s + SQUARES_AHEAD)
+            if hq == 0 and c + 1 < PASSES:
+                group_x(c + 1)
+            rh = work.tile([P, PACK, H_ROUND], F32)
+            nc.vector.scalar_tensor_tensor(
+                out=rh[:],
+                in0=rc2[:],
+                scalar=0.25,
+                in1=minus_h_n[:, h_cols].unsqueeze(1).to_broadcast([P, PACK, H_ROUND]),
+                op0=ALU.subtract,
+                op1=ALU.mult,
+            )
+            dz_words = grouped.tile([P, H_ROUND, PACK], BF16, align_bytes=64)
+            nc.vector.tensor_tensor(
+                out=words_in_fours(dz_words[:]),
+                in0=rows_in_fours(w[:]),
+                in1=rows_in_fours(nz[:]),
+                op=ALU.mult,
+            )
+            dr_words = grouped.tile([P, H_ROUND, PACK], BF16, align_bytes=64)
+            nc.vector.tensor_tensor(
+                out=words_in_fours(dr_words[:]),
+                in0=rows_in_fours(rh[:]),
+                in1=rows_in_fours(d_n[:]),
+                op=ALU.mult,
+            )
+
+            if hq == 0:
+                nc.vector.quantize_mx(
+                    out=x_codes[:, c, :].bitcast(E4M3_X4),
+                    scales=x_scales[:, c, :],
+                    in_=x_grouped[c][:].rearrange("p w j -> p (w j)"),
+                )
+            if c == 0:
+                for gate in range(GATES):
                     for half in range(HALVES):
-                        m_cols = slice(half * M_TILE, (half + 1) * M_TILE)
-                        nc.tensor.matmul_mx(
-                            out=acc[gate][half][:],
-                            lhsT=codes[:, gate, m_cols].bitcast(E5M2_X4),
-                            lhsT_scale=scales[:, gate, m_cols],
-                            rhs=x_codes[:, c, :].bitcast(E4M3_X4),
-                            rhs_scale=x_scales[:, c, :],
-                            start=(c == 0),
-                            stop=(c == PASSES - 1),
-                        )
-
+                        acc[gate, half] = psum.tile([M_TILE, I], F32, name="acc", tag="acc")
+            codes = packed.tile([P, GATES, H_ROUND], U32, align_bytes=64)
+            scales = packed.tile([P, GATES, H_ROUND], U8, align_bytes=64)
+            words_of = {0: dr_words, 1: dz_words, 2: dn_words}
             for gate in GATE_ORDER:
+                nc.vector.quantize_mx(
+                    out=codes[:, gate, :].bitcast(E5M2_X4),
+                    scales=scales[:, gate, :],
+                    in_=words_of[gate][:].rearrange("p w j -> p (w j)"),
+                )
                 for half in range(HALVES):
-                    row0 = gate * H + hq * H_ROUND + half * M_TILE
-                    res = results.tile([M_TILE, I], F32)
-                    if hq == ROUNDS - 1 and gate == GATE_ORDER[-1] and half == HALVES - 1:
-                        nc.vector.tensor_copy(out=res[:], in_=acc[gate][half][:])
+                    m_cols = slice(half * M_TILE, (half + 1) * M_TILE)
+                    nc.tensor.matmul_mx(
+                        out=acc[gate, half][:],
+                        lhsT=codes[:, gate, m_cols].bitcast(E5M2_X4),
+                        lhsT_scale=scales[:, gate, m_cols],
+                        rhs=x_codes[:, c, :].bitcast(E4M3_X4),
+                        rhs_scale=x_scales[:, c, :],
+                        start=(c == 0),
+                        stop=(c == PASSES - 1),
+                    )
+
+            if c == PASSES - 1:
+                for gate in GATE_ORDER:
+                    for half in range(HALVES):
+                        row0 = gate * H + hq * H_ROUND + half * M_TILE
+                        res = results.tile([M_TILE, I], F32)
+                        if s == STEPS - 1 and gate == GATE_ORDER[-1] and half == HALVES - 1:
+                            nc.vector.tensor_copy(out=res[:], in_=acc[gate, half][:])
+                        else:
+                            nc.scalar.copy(out=res[:], in_=acc[gate, half][:])
                         nc.sync.dma_start(out=out[row0 : row0 + M_TILE, :], in_=res[:])
-                    else:
-                        nc.scalar.copy(out=res[:], in_=acc[gate][half][:])
-                        nc.scalar.dma_start(out=out[row0 : row0 + M_TILE, :], in_=res[:])

@@ -1,6 +1,7 @@
 from contextlib import ExitStack
 
 import concourse.mybir as mybir
+from concourse.masks import make_identity
 
 F32 = mybir.dt.float32
 BF16 = mybir.dt.bfloat16
@@ -22,7 +23,8 @@ H_ROUND = 256
 ROUNDS = H // H_ROUND
 HALVES = H_ROUND // M_TILE
 STEPS = ROUNDS * PASSES
-LOADS_AHEAD = 3
+N_MAX = 512
+LOADS_AHEAD = 5
 SQUARES_AHEAD = 2
 
 FLOPS = 2 * T * B * GATES * H * I
@@ -47,34 +49,39 @@ def tile_grucellmodel_pa_v_kernel(tc, input_seq, W_ih, b_ih, gh, r, z, n, grad_o
         grouped = ctx.enter_context(tc.tile_pool(name="grouped", bufs=2))
         packed = ctx.enter_context(tc.tile_pool(name="packed", bufs=2))
         results = ctx.enter_context(tc.tile_pool(name="results", bufs=GATES * HALVES))
-        psum = ctx.enter_context(tc.psum_pool(name="psum", bufs=8))
+        psum = ctx.enter_context(tc.psum_pool(name="psum", bufs=GATES * HALVES))
+        psum_operands = ctx.enter_context(tc.psum_pool(name="psum_operands", bufs=1))
         ctx.enter_context(tc.manual_schedule())
 
         h_n = keep.tile([P, H], BF16)
         minus_h_n = keep.tile([P, H], BF16)
         minus_half = keep.tile([P, 1], F32)
+        identity = keep.tile([P, P], BF16)
+        minus_h_n_psum = psum_operands.tile([P, H], BF16)
         x_rows = keep.tile([P, PASSES, PACK, I], BF16)
         x_codes = keep.tile([P, PASSES, I], U32, align_bytes=64)
         x_scales = keep.tile([P, PASSES, I], U8, align_bytes=64)
         loaded = {}
         squared = {}
         x_grouped = {}
+        g_psum = {}
+        n_times_z = {}
 
         def load(s):
             hq, c = divmod(s, PASSES)
             steps = slice(c * PACK, (c + 1) * PACK)
             h_cols = slice(hq * H_ROUND, (hq + 1) * H_ROUND)
-            z_t = loads.tile([P, PACK, H_ROUND], F32)
-            nc.sync.dma_start(out=z_t[:], in_=z[steps, :, h_cols].rearrange("j b h -> b j h"))
             g_t = loads.tile([P, PACK, H_ROUND], BF16)
             nc.sync.dma_start(out=g_t[:], in_=grad_out[:, steps, h_cols])
-            n_t = loads.tile([P, PACK, H_ROUND], F32)
-            nc.sync.dma_start(out=n_t[:], in_=n[steps, :, h_cols].rearrange("j b h -> b j h"))
-            r_t = loads.tile([P, PACK, H_ROUND], F32)
-            nc.sync.dma_start(out=r_t[:], in_=r[steps, :, h_cols].rearrange("j b h -> b j h"))
-            loaded[s] = (z_t, g_t, n_t, r_t)
+            z_t = loads.tile([P, PACK, H_ROUND], F32)
+            nc.sync.dma_start(out=z_t[:], in_=z[steps, :, h_cols].rearrange("j b h -> b j h"))
             if s == 0:
                 nc.sync.dma_start(out=h_n[:], in_=gh[:, 2 * H : 3 * H])
+            r_t = loads.tile([P, PACK, H_ROUND], F32)
+            nc.sync.dma_start(out=r_t[:], in_=r[steps, :, h_cols].rearrange("j b h -> b j h"))
+            n_t = loads.tile([P, PACK, H_ROUND], F32)
+            nc.sync.dma_start(out=n_t[:], in_=n[steps, :, h_cols].rearrange("j b h -> b j h"))
+            loaded[s] = (z_t, g_t, n_t, r_t)
             if hq == 0:
                 nc.sync.dma_start(
                     out=x_rows[:, c, :, :], in_=input_seq[steps].rearrange("j b i -> b j i")
@@ -82,11 +89,33 @@ def tile_grucellmodel_pa_v_kernel(tc, input_seq, W_ih, b_ih, gh, r, z, n, grad_o
 
         def square(s):
             z_t, g_t, n_t, r_t = loaded[s]
-            nn = ahead.tile([P, PACK, H_ROUND], F32)
-            nc.scalar.activation(out=nn[:], in_=n_t[:], func=ACT.Square)
             rc2 = ahead.tile([P, PACK, H_ROUND], F32)
             nc.scalar.activation(out=rc2[:], in_=r_t[:], func=ACT.Square, bias=minus_half[:])
+            nn = ahead.tile([P, PACK, H_ROUND], F32)
+            nc.scalar.activation(out=nn[:], in_=n_t[:], func=ACT.Square)
             squared[s] = (nn, rc2)
+
+        def copy_into_psum(dst, src):
+            for col0 in range(0, dst.shape[1], N_MAX):
+                nc.tensor.matmul(
+                    out=dst[:, col0 : col0 + N_MAX],
+                    lhsT=identity[:],
+                    rhs=src[:, col0 : col0 + N_MAX],
+                    start=True,
+                    stop=True,
+                )
+
+        def copy_g(s):
+            z_t, g_t, n_t, r_t = loaded[s]
+            g_p = psum_operands.tile([P, PACK * H_ROUND], BF16)
+            copy_into_psum(g_p[:], g_t[:].rearrange("p j h -> p (j h)"))
+            g_psum[s] = g_p
+
+        def multiply_n_z(s):
+            z_t, g_t, n_t, r_t = loaded[s]
+            nz = ahead.tile([P, PACK, H_ROUND], F32)
+            nc.gpsimd.tensor_tensor(out=nz[:], in0=n_t[:], in1=z_t[:], op=ALU.mult)
+            n_times_z[s] = nz
 
         def group_x(c):
             x_words = grouped.tile([P, I, PACK], BF16, align_bytes=64)
@@ -94,10 +123,14 @@ def tile_grucellmodel_pa_v_kernel(tc, input_seq, W_ih, b_ih, gh, r, z, n, grad_o
             x_grouped[c] = x_words
 
         nc.vector.memset(minus_half[:], -0.5)
+        make_identity(nc, identity[:])
         for s in range(LOADS_AHEAD):
             load(s)
-        square(0)
+        copy_g(0)
         nc.scalar.mul(out=minus_h_n[:], in_=h_n[:], mul=-1.0)
+        copy_into_psum(minus_h_n_psum[:], minus_h_n[:])
+        square(0)
+        multiply_n_z(0)
         group_x(0)
         square(1)
 
@@ -109,13 +142,30 @@ def tile_grucellmodel_pa_v_kernel(tc, input_seq, W_ih, b_ih, gh, r, z, n, grad_o
                 load(s + LOADS_AHEAD)
             z_t, g_t, n_t, r_t = loaded[s]
             nn, rc2 = squared[s]
+            nz = n_times_z[s]
+            if s + 1 < STEPS:
+                multiply_n_z(s + 1)
 
             w = work.tile([P, PACK, H_ROUND], F32)
             nc.vector.scalar_tensor_tensor(
-                out=w[:], in0=z_t[:], scalar=1.0, in1=g_t[:], op0=ALU.subtract, op1=ALU.mult
+                out=w[:],
+                in0=z_t[:],
+                scalar=1.0,
+                in1=g_psum[s][:].rearrange("p (j h) -> p j h", j=PACK),
+                op0=ALU.subtract,
+                op1=ALU.mult,
             )
-            nz = work.tile([P, PACK, H_ROUND], F32)
-            nc.vector.tensor_tensor(out=nz[:], in0=n_t[:], in1=z_t[:], op=ALU.mult)
+            if s + 1 < STEPS:
+                copy_g(s + 1)
+            rh = work.tile([P, PACK, H_ROUND], F32)
+            nc.vector.scalar_tensor_tensor(
+                out=rh[:],
+                in0=rc2[:],
+                scalar=0.25,
+                in1=minus_h_n_psum[:, h_cols].unsqueeze(1).to_broadcast([P, PACK, H_ROUND]),
+                op0=ALU.subtract,
+                op1=ALU.mult,
+            )
             d_n = work.tile([P, PACK, H_ROUND], F32)
             nc.vector.scalar_tensor_tensor(
                 out=d_n[:], in0=nn[:], scalar=1.0, in1=w[:], op0=ALU.subtract, op1=ALU.mult
@@ -126,15 +176,6 @@ def tile_grucellmodel_pa_v_kernel(tc, input_seq, W_ih, b_ih, gh, r, z, n, grad_o
                 square(s + SQUARES_AHEAD)
             if hq == 0 and c + 1 < PASSES:
                 group_x(c + 1)
-            rh = work.tile([P, PACK, H_ROUND], F32)
-            nc.vector.scalar_tensor_tensor(
-                out=rh[:],
-                in0=rc2[:],
-                scalar=0.25,
-                in1=minus_h_n[:, h_cols].unsqueeze(1).to_broadcast([P, PACK, H_ROUND]),
-                op0=ALU.subtract,
-                op1=ALU.mult,
-            )
             dz_words = grouped.tile([P, H_ROUND, PACK], BF16, align_bytes=64)
             nc.vector.tensor_tensor(
                 out=words_in_fours(dz_words[:]),

@@ -17,7 +17,7 @@ P = 128
 PACK = 4
 PASSES = T // PACK
 GATES = 3
-GATE_ORDER = (1, 2, 0)
+D_R, D_Z, D_N = 0, 1, 2
 M_TILE = 128
 H_ROUND = 256
 ROUNDS = H // H_ROUND
@@ -26,6 +26,7 @@ STEPS = ROUNDS * PASSES
 N_MAX = 512
 LOADS_AHEAD = 5
 SQUARES_AHEAD = 2
+GPSIMD_COLS = 64
 
 FLOPS = 2 * T * B * GATES * H * I
 BYTES = T * B * I * 2 + B * H * 2 + 3 * T * B * H * 4 + B * T * H * 2 + GATES * H * I * 4
@@ -37,6 +38,10 @@ def rows_in_fours(rows):
 
 def words_in_fours(words):
     return words.rearrange("p (c i) j -> p c j i", i=4)
+
+
+def rows_by_column(rows):
+    return rows.rearrange("p j w -> p w j")
 
 
 def tile_grucellmodel_pa_v_kernel(tc, input_seq, W_ih, b_ih, gh, r, z, n, grad_out, out):
@@ -65,7 +70,10 @@ def tile_grucellmodel_pa_v_kernel(tc, input_seq, W_ih, b_ih, gh, r, z, n, grad_o
         squared = {}
         x_grouped = {}
         g_psum = {}
-        n_times_z = {}
+        factors = {}
+        d_n_of = {}
+        words = {}
+        acc = {}
 
         def load(s):
             hq, c = divmod(s, PASSES)
@@ -73,14 +81,14 @@ def tile_grucellmodel_pa_v_kernel(tc, input_seq, W_ih, b_ih, gh, r, z, n, grad_o
             h_cols = slice(hq * H_ROUND, (hq + 1) * H_ROUND)
             g_t = loads.tile([P, PACK, H_ROUND], BF16)
             nc.sync.dma_start(out=g_t[:], in_=grad_out[:, steps, h_cols])
+            n_t = loads.tile([P, PACK, H_ROUND], F32)
+            nc.sync.dma_start(out=n_t[:], in_=n[steps, :, h_cols].rearrange("j b h -> b j h"))
             z_t = loads.tile([P, PACK, H_ROUND], F32)
             nc.sync.dma_start(out=z_t[:], in_=z[steps, :, h_cols].rearrange("j b h -> b j h"))
             if s == 0:
                 nc.sync.dma_start(out=h_n[:], in_=gh[:, 2 * H : 3 * H])
             r_t = loads.tile([P, PACK, H_ROUND], F32)
             nc.sync.dma_start(out=r_t[:], in_=r[steps, :, h_cols].rearrange("j b h -> b j h"))
-            n_t = loads.tile([P, PACK, H_ROUND], F32)
-            nc.sync.dma_start(out=n_t[:], in_=n[steps, :, h_cols].rearrange("j b h -> b j h"))
             loaded[s] = (z_t, g_t, n_t, r_t)
             if hq == 0:
                 nc.sync.dma_start(
@@ -89,11 +97,16 @@ def tile_grucellmodel_pa_v_kernel(tc, input_seq, W_ih, b_ih, gh, r, z, n, grad_o
 
         def square(s):
             z_t, g_t, n_t, r_t = loaded[s]
-            rc2 = ahead.tile([P, PACK, H_ROUND], F32)
-            nc.scalar.activation(out=rc2[:], in_=r_t[:], func=ACT.Square, bias=minus_half[:])
             nn = ahead.tile([P, PACK, H_ROUND], F32)
             nc.scalar.activation(out=nn[:], in_=n_t[:], func=ACT.Square)
-            squared[s] = (nn, rc2)
+            zc2 = ahead.tile([P, PACK, H_ROUND], F32)
+            nc.scalar.activation(out=zc2[:], in_=z_t[:], func=ACT.Square, bias=minus_half[:])
+            if s == 0:
+                nc.scalar.mul(out=minus_h_n[:], in_=h_n[:], mul=-1.0)
+                copy_into_psum(minus_h_n_psum[:], minus_h_n[:])
+            rc2 = ahead.tile([P, PACK, H_ROUND], F32)
+            nc.scalar.activation(out=rc2[:], in_=r_t[:], func=ACT.Square, bias=minus_half[:])
+            squared[s] = (nn, zc2, rc2)
 
         def copy_into_psum(dst, src):
             for col0 in range(0, dst.shape[1], N_MAX):
@@ -111,49 +124,23 @@ def tile_grucellmodel_pa_v_kernel(tc, input_seq, W_ih, b_ih, gh, r, z, n, grad_o
             copy_into_psum(g_p[:], g_t[:].rearrange("p j h -> p (j h)"))
             g_psum[s] = g_p
 
-        def multiply_n_z(s):
-            z_t, g_t, n_t, r_t = loaded[s]
-            nz = ahead.tile([P, PACK, H_ROUND], F32)
-            nc.gpsimd.tensor_tensor(out=nz[:], in0=n_t[:], in1=z_t[:], op=ALU.mult)
-            n_times_z[s] = nz
-
         def group_x(c):
             x_words = grouped.tile([P, I, PACK], BF16, align_bytes=64)
             nc.scalar.copy(out=words_in_fours(x_words[:]), in_=rows_in_fours(x_rows[:, c, :, :]))
             x_grouped[c] = x_words
 
-        nc.vector.memset(minus_half[:], -0.5)
-        make_identity(nc, identity[:])
-        for s in range(LOADS_AHEAD):
-            load(s)
-        copy_g(0)
-        nc.scalar.mul(out=minus_h_n[:], in_=h_n[:], mul=-1.0)
-        copy_into_psum(minus_h_n_psum[:], minus_h_n[:])
-        square(0)
-        multiply_n_z(0)
-        group_x(0)
-        square(1)
-
-        acc = {}
-        for s in range(STEPS):
+        def multiply_from_psum(s):
             hq, c = divmod(s, PASSES)
             h_cols = slice(hq * H_ROUND, (hq + 1) * H_ROUND)
-            if s + LOADS_AHEAD < STEPS:
-                load(s + LOADS_AHEAD)
-            z_t, g_t, n_t, r_t = loaded[s]
-            nn, rc2 = squared[s]
-            nz = n_times_z[s]
-            if s + 1 < STEPS:
-                multiply_n_z(s + 1)
-
-            w = work.tile([P, PACK, H_ROUND], F32)
+            nn, zc2, rc2 = squared[s]
+            g_rows = g_psum[s][:].rearrange("p (j h) -> p j h", j=PACK)
+            gn = work.tile([P, PACK, H_ROUND], F32)
             nc.vector.scalar_tensor_tensor(
-                out=w[:],
-                in0=z_t[:],
-                scalar=1.0,
-                in1=g_psum[s][:].rearrange("p (j h) -> p j h", j=PACK),
-                op0=ALU.subtract,
-                op1=ALU.mult,
+                out=gn[:], in0=nn[:], scalar=1.0, in1=g_rows, op0=ALU.subtract, op1=ALU.mult
+            )
+            gz = work.tile([P, PACK, H_ROUND], F32)
+            nc.vector.scalar_tensor_tensor(
+                out=gz[:], in0=zc2[:], scalar=0.25, in1=g_rows, op0=ALU.subtract, op1=ALU.mult
             )
             if s + 1 < STEPS:
                 copy_g(s + 1)
@@ -166,69 +153,129 @@ def tile_grucellmodel_pa_v_kernel(tc, input_seq, W_ih, b_ih, gh, r, z, n, grad_o
                 op0=ALU.subtract,
                 op1=ALU.mult,
             )
+            factors[s] = (gn, gz, rh)
+
+        def finish_d_n(s):
+            z_t, g_t, n_t, r_t = loaded[s]
+            gn, gz, rh = factors[s]
             d_n = work.tile([P, PACK, H_ROUND], F32)
             nc.vector.scalar_tensor_tensor(
-                out=d_n[:], in0=nn[:], scalar=1.0, in1=w[:], op0=ALU.subtract, op1=ALU.mult
+                out=d_n[:], in0=z_t[:], scalar=1.0, in1=gn[:], op0=ALU.subtract, op1=ALU.mult
             )
+            d_n_of[s] = d_n
             dn_words = grouped.tile([P, H_ROUND, PACK], BF16, align_bytes=64)
             nc.scalar.copy(out=words_in_fours(dn_words[:]), in_=rows_in_fours(d_n[:]))
+            words[s, D_N] = dn_words
+            words[s, D_R] = grouped.tile([P, H_ROUND, PACK], BF16, align_bytes=64, name="dr_words")
+            words[s, D_Z] = grouped.tile([P, H_ROUND, PACK], BF16, align_bytes=64, name="dz_words")
+
+        def gpsimd_share(s):
+            z_t, g_t, n_t, r_t = loaded[s]
+            gn, gz, rh = factors[s]
+            nc.gpsimd.tensor_tensor(
+                out=words[s, D_R][:, :GPSIMD_COLS, :],
+                in0=rows_by_column(rh[:, :, :GPSIMD_COLS]),
+                in1=rows_by_column(d_n_of[s][:, :, :GPSIMD_COLS]),
+                op=ALU.mult,
+            )
+            nc.gpsimd.tensor_tensor(
+                out=words[s, D_Z][:], in0=rows_by_column(gz[:]), in1=rows_by_column(n_t[:]), op=ALU.mult
+            )
+
+        def vector_d_r(s, col0):
+            gn, gz, rh = factors[s]
+            nc.vector.tensor_tensor(
+                out=words_in_fours(words[s, D_R][:, col0:, :]),
+                in0=rows_in_fours(rh[:, :, col0:]),
+                in1=rows_in_fours(d_n_of[s][:, :, col0:]),
+                op=ALU.mult,
+            )
+
+        def vector_d_z(s):
+            z_t, g_t, n_t, r_t = loaded[s]
+            gn, gz, rh = factors[s]
+            nc.vector.tensor_tensor(
+                out=words_in_fours(words[s, D_Z][:]),
+                in0=rows_in_fours(gz[:]),
+                in1=rows_in_fours(n_t[:]),
+                op=ALU.mult,
+            )
+
+        def quantise_x(c):
+            nc.vector.quantize_mx(
+                out=x_codes[:, c, :].bitcast(E4M3_X4),
+                scales=x_scales[:, c, :],
+                in_=x_grouped[c][:].rearrange("p w j -> p (w j)"),
+            )
+
+        def quantise_and_multiply(s, gate):
+            hq, c = divmod(s, PASSES)
+            codes = packed.tile([P, H_ROUND], U32, align_bytes=64, name="codes", tag="codes%d" % gate)
+            scales = packed.tile([P, H_ROUND], U8, align_bytes=64, name="scales", tag="scales%d" % gate)
+            nc.vector.quantize_mx(
+                out=codes[:].bitcast(E5M2_X4),
+                scales=scales[:],
+                in_=words[s, gate][:].rearrange("p w j -> p (w j)"),
+            )
+            for half in range(HALVES):
+                if c == 0:
+                    acc[gate, half] = psum.tile([M_TILE, I], F32, name="acc", tag="acc")
+                m_cols = slice(half * M_TILE, (half + 1) * M_TILE)
+                nc.tensor.matmul_mx(
+                    out=acc[gate, half][:],
+                    lhsT=codes[:, m_cols].bitcast(E5M2_X4),
+                    lhsT_scale=scales[:, m_cols],
+                    rhs=x_codes[:, c, :].bitcast(E4M3_X4),
+                    rhs_scale=x_scales[:, c, :],
+                    start=(c == 0),
+                    stop=(c == PASSES - 1),
+                )
+
+        def store(s, gate, on_vector):
+            hq, c = divmod(s, PASSES)
+            for half in range(HALVES):
+                row0 = gate * H + hq * H_ROUND + half * M_TILE
+                res = results.tile([M_TILE, I], F32)
+                if on_vector and half == HALVES - 1:
+                    nc.vector.tensor_copy(out=res[:], in_=acc[gate, half][:])
+                else:
+                    nc.scalar.copy(out=res[:], in_=acc[gate, half][:])
+                nc.sync.dma_start(out=out[row0 : row0 + M_TILE, :], in_=res[:])
+
+        nc.vector.memset(minus_half[:], -0.5)
+        make_identity(nc, identity[:])
+        for s in range(LOADS_AHEAD):
+            load(s)
+        copy_g(0)
+        square(0)
+        group_x(0)
+        square(1)
+
+        LAST = STEPS - 1
+        for s in range(STEPS):
+            hq, c = divmod(s, PASSES)
+            if s + LOADS_AHEAD < STEPS:
+                load(s + LOADS_AHEAD)
+            multiply_from_psum(s)
+            if s > 0:
+                before = s - 1
+                vector_d_r(before, GPSIMD_COLS)
+                if before < PASSES:
+                    quantise_x(before)
+                for gate in (D_N, D_R, D_Z):
+                    quantise_and_multiply(before, gate)
+                if c == 0:
+                    for gate in (D_N, D_R, D_Z):
+                        store(before, gate, False)
+            finish_d_n(s)
+            if s < LAST:
+                gpsimd_share(s)
             if s + SQUARES_AHEAD < STEPS:
                 square(s + SQUARES_AHEAD)
             if hq == 0 and c + 1 < PASSES:
                 group_x(c + 1)
-            dz_words = grouped.tile([P, H_ROUND, PACK], BF16, align_bytes=64)
-            nc.vector.tensor_tensor(
-                out=words_in_fours(dz_words[:]),
-                in0=rows_in_fours(w[:]),
-                in1=rows_in_fours(nz[:]),
-                op=ALU.mult,
-            )
-            dr_words = grouped.tile([P, H_ROUND, PACK], BF16, align_bytes=64)
-            nc.vector.tensor_tensor(
-                out=words_in_fours(dr_words[:]),
-                in0=rows_in_fours(rh[:]),
-                in1=rows_in_fours(d_n[:]),
-                op=ALU.mult,
-            )
-
-            if hq == 0:
-                nc.vector.quantize_mx(
-                    out=x_codes[:, c, :].bitcast(E4M3_X4),
-                    scales=x_scales[:, c, :],
-                    in_=x_grouped[c][:].rearrange("p w j -> p (w j)"),
-                )
-            if c == 0:
-                for gate in range(GATES):
-                    for half in range(HALVES):
-                        acc[gate, half] = psum.tile([M_TILE, I], F32, name="acc", tag="acc")
-            codes = packed.tile([P, GATES, H_ROUND], U32, align_bytes=64)
-            scales = packed.tile([P, GATES, H_ROUND], U8, align_bytes=64)
-            words_of = {0: dr_words, 1: dz_words, 2: dn_words}
-            for gate in GATE_ORDER:
-                nc.vector.quantize_mx(
-                    out=codes[:, gate, :].bitcast(E5M2_X4),
-                    scales=scales[:, gate, :],
-                    in_=words_of[gate][:].rearrange("p w j -> p (w j)"),
-                )
-                for half in range(HALVES):
-                    m_cols = slice(half * M_TILE, (half + 1) * M_TILE)
-                    nc.tensor.matmul_mx(
-                        out=acc[gate, half][:],
-                        lhsT=codes[:, gate, m_cols].bitcast(E5M2_X4),
-                        lhsT_scale=scales[:, gate, m_cols],
-                        rhs=x_codes[:, c, :].bitcast(E4M3_X4),
-                        rhs_scale=x_scales[:, c, :],
-                        start=(c == 0),
-                        stop=(c == PASSES - 1),
-                    )
-
-            if c == PASSES - 1:
-                for gate in GATE_ORDER:
-                    for half in range(HALVES):
-                        row0 = gate * H + hq * H_ROUND + half * M_TILE
-                        res = results.tile([M_TILE, I], F32)
-                        if s == STEPS - 1 and gate == GATE_ORDER[-1] and half == HALVES - 1:
-                            nc.vector.tensor_copy(out=res[:], in_=acc[gate, half][:])
-                        else:
-                            nc.scalar.copy(out=res[:], in_=acc[gate, half][:])
-                        nc.sync.dma_start(out=out[row0 : row0 + M_TILE, :], in_=res[:])
+        vector_d_z(LAST)
+        vector_d_r(LAST, 0)
+        for gate in (D_Z, D_N, D_R):
+            quantise_and_multiply(LAST, gate)
+            store(LAST, gate, gate == D_R)

@@ -40,10 +40,6 @@ def words_in_fours(words):
     return words.rearrange("p (c i) j -> p c j i", i=4)
 
 
-def rows_by_column(rows):
-    return rows.rearrange("p j w -> p w j")
-
-
 def tile_grucellmodel_pa_v_kernel(tc, input_seq, W_ih, b_ih, gh, r, z, n, grad_out, out):
     nc = tc.nc
     with ExitStack() as ctx:
@@ -173,13 +169,16 @@ def tile_grucellmodel_pa_v_kernel(tc, input_seq, W_ih, b_ih, gh, r, z, n, grad_o
             z_t, g_t, n_t, r_t = loaded[s]
             gn, gz, rh = factors[s]
             nc.gpsimd.tensor_tensor(
-                out=words[s, D_R][:, :GPSIMD_COLS, :],
-                in0=rows_by_column(rh[:, :, :GPSIMD_COLS]),
-                in1=rows_by_column(d_n_of[s][:, :, :GPSIMD_COLS]),
+                out=words_in_fours(words[s, D_R][:, :GPSIMD_COLS, :]),
+                in0=rows_in_fours(rh[:, :, :GPSIMD_COLS]),
+                in1=rows_in_fours(d_n_of[s][:, :, :GPSIMD_COLS]),
                 op=ALU.mult,
             )
             nc.gpsimd.tensor_tensor(
-                out=words[s, D_Z][:], in0=rows_by_column(gz[:]), in1=rows_by_column(n_t[:]), op=ALU.mult
+                out=words_in_fours(words[s, D_Z][:]),
+                in0=rows_in_fours(gz[:]),
+                in1=rows_in_fours(n_t[:]),
+                op=ALU.mult,
             )
 
         def vector_d_r(s, col0):

@@ -26,6 +26,7 @@ STEPS = ROUNDS * PASSES
 N_MAX = 512
 LOADS_AHEAD = 5
 SQUARES_AHEAD = 2
+X_LATE = 2
 GPSIMD_COLS = 64
 
 FLOPS = 2 * T * B * GATES * H * I
@@ -48,16 +49,17 @@ def tile_grucellmodel_pa_v_kernel(tc, input_seq, W_ih, b_ih, gh, r, z, n, grad_o
         ahead = ctx.enter_context(tc.tile_pool(name="ahead", bufs=SQUARES_AHEAD + 1))
         work = ctx.enter_context(tc.tile_pool(name="work", bufs=2))
         grouped = ctx.enter_context(tc.tile_pool(name="grouped", bufs=2))
-        packed = ctx.enter_context(tc.tile_pool(name="packed", bufs=2))
+        packed = ctx.enter_context(tc.tile_pool(name="packed", bufs=X_LATE + 2))
         results = ctx.enter_context(tc.tile_pool(name="results", bufs=GATES * HALVES))
         psum = ctx.enter_context(tc.psum_pool(name="psum", bufs=GATES * HALVES))
         psum_operands = ctx.enter_context(tc.psum_pool(name="psum_operands", bufs=1))
         ctx.enter_context(tc.manual_schedule())
 
         h_n = keep.tile([P, H], BF16)
-        minus_h_n = keep.tile([P, H], BF16)
         minus_half = keep.tile([P, 1], F32)
+        warm_up = keep.tile([P, 1], F32)
         identity = keep.tile([P, P], BF16)
+        minus_identity = keep.tile([P, P], BF16)
         minus_h_n_psum = psum_operands.tile([P, H], BF16)
         x_rows = keep.tile([P, PASSES, PACK, I], BF16)
         x_codes = keep.tile([P, PASSES, I], U32, align_bytes=64)
@@ -69,6 +71,7 @@ def tile_grucellmodel_pa_v_kernel(tc, input_seq, W_ih, b_ih, gh, r, z, n, grad_o
         factors = {}
         d_n_of = {}
         words = {}
+        quantised = {}
         acc = {}
 
         def load(s):
@@ -77,38 +80,35 @@ def tile_grucellmodel_pa_v_kernel(tc, input_seq, W_ih, b_ih, gh, r, z, n, grad_o
             h_cols = slice(hq * H_ROUND, (hq + 1) * H_ROUND)
             g_t = loads.tile([P, PACK, H_ROUND], BF16)
             nc.sync.dma_start(out=g_t[:], in_=grad_out[:, steps, h_cols])
-            n_t = loads.tile([P, PACK, H_ROUND], F32)
-            nc.sync.dma_start(out=n_t[:], in_=n[steps, :, h_cols].rearrange("j b h -> b j h"))
             z_t = loads.tile([P, PACK, H_ROUND], F32)
             nc.sync.dma_start(out=z_t[:], in_=z[steps, :, h_cols].rearrange("j b h -> b j h"))
             if s == 0:
                 nc.sync.dma_start(out=h_n[:], in_=gh[:, 2 * H : 3 * H])
             r_t = loads.tile([P, PACK, H_ROUND], F32)
             nc.sync.dma_start(out=r_t[:], in_=r[steps, :, h_cols].rearrange("j b h -> b j h"))
+            n_t = loads.tile([P, PACK, H_ROUND], F32)
+            nc.sync.dma_start(out=n_t[:], in_=n[steps, :, h_cols].rearrange("j b h -> b j h"))
             loaded[s] = (z_t, g_t, n_t, r_t)
-            if hq == 0:
-                nc.sync.dma_start(
-                    out=x_rows[:, c, :, :], in_=input_seq[steps].rearrange("j b i -> b j i")
-                )
+
+        def load_x(c):
+            steps = slice(c * PACK, (c + 1) * PACK)
+            nc.sync.dma_start(out=x_rows[:, c, :, :], in_=input_seq[steps].rearrange("j b i -> b j i"))
 
         def square(s):
             z_t, g_t, n_t, r_t = loaded[s]
-            nn = ahead.tile([P, PACK, H_ROUND], F32)
-            nc.scalar.activation(out=nn[:], in_=n_t[:], func=ACT.Square)
             zc2 = ahead.tile([P, PACK, H_ROUND], F32)
             nc.scalar.activation(out=zc2[:], in_=z_t[:], func=ACT.Square, bias=minus_half[:])
-            if s == 0:
-                nc.scalar.mul(out=minus_h_n[:], in_=h_n[:], mul=-1.0)
-                copy_into_psum(minus_h_n_psum[:], minus_h_n[:])
             rc2 = ahead.tile([P, PACK, H_ROUND], F32)
             nc.scalar.activation(out=rc2[:], in_=r_t[:], func=ACT.Square, bias=minus_half[:])
+            nn = ahead.tile([P, PACK, H_ROUND], F32)
+            nc.scalar.activation(out=nn[:], in_=n_t[:], func=ACT.Square)
             squared[s] = (nn, zc2, rc2)
 
-        def copy_into_psum(dst, src):
+        def copy_into_psum(dst, src, diagonal):
             for col0 in range(0, dst.shape[1], N_MAX):
                 nc.tensor.matmul(
                     out=dst[:, col0 : col0 + N_MAX],
-                    lhsT=identity[:],
+                    lhsT=diagonal[:],
                     rhs=src[:, col0 : col0 + N_MAX],
                     start=True,
                     stop=True,
@@ -117,7 +117,7 @@ def tile_grucellmodel_pa_v_kernel(tc, input_seq, W_ih, b_ih, gh, r, z, n, grad_o
         def copy_g(s):
             z_t, g_t, n_t, r_t = loaded[s]
             g_p = psum_operands.tile([P, PACK * H_ROUND], BF16)
-            copy_into_psum(g_p[:], g_t[:].rearrange("p j h -> p (j h)"))
+            copy_into_psum(g_p[:], g_t[:].rearrange("p j h -> p (j h)"), identity)
             g_psum[s] = g_p
 
         def group_x(c):
@@ -132,7 +132,7 @@ def tile_grucellmodel_pa_v_kernel(tc, input_seq, W_ih, b_ih, gh, r, z, n, grad_o
             g_rows = g_psum[s][:].rearrange("p (j h) -> p j h", j=PACK)
             gn = work.tile([P, PACK, H_ROUND], F32)
             nc.vector.scalar_tensor_tensor(
-                out=gn[:], in0=nn[:], scalar=1.0, in1=g_rows, op0=ALU.subtract, op1=ALU.mult
+                out=gn[:], in0=loaded[s][0][:], scalar=1.0, in1=g_rows, op0=ALU.subtract, op1=ALU.mult
             )
             gz = work.tile([P, PACK, H_ROUND], F32)
             nc.vector.scalar_tensor_tensor(
@@ -152,11 +152,11 @@ def tile_grucellmodel_pa_v_kernel(tc, input_seq, W_ih, b_ih, gh, r, z, n, grad_o
             factors[s] = (gn, gz, rh)
 
         def finish_d_n(s):
-            z_t, g_t, n_t, r_t = loaded[s]
+            nn, zc2, rc2 = squared[s]
             gn, gz, rh = factors[s]
             d_n = work.tile([P, PACK, H_ROUND], F32)
             nc.vector.scalar_tensor_tensor(
-                out=d_n[:], in0=z_t[:], scalar=1.0, in1=gn[:], op0=ALU.subtract, op1=ALU.mult
+                out=d_n[:], in0=nn[:], scalar=1.0, in1=gn[:], op0=ALU.subtract, op1=ALU.mult
             )
             d_n_of[s] = d_n
             dn_words = grouped.tile([P, H_ROUND, PACK], BF16, align_bytes=64)
@@ -207,8 +207,7 @@ def tile_grucellmodel_pa_v_kernel(tc, input_seq, W_ih, b_ih, gh, r, z, n, grad_o
                 in_=x_grouped[c][:].rearrange("p w j -> p (w j)"),
             )
 
-        def quantise_and_multiply(s, gate):
-            hq, c = divmod(s, PASSES)
+        def quantise(s, gate):
             codes = packed.tile([P, H_ROUND], U32, align_bytes=64, name="codes", tag="codes%d" % gate)
             scales = packed.tile([P, H_ROUND], U8, align_bytes=64, name="scales", tag="scales%d" % gate)
             nc.vector.quantize_mx(
@@ -216,6 +215,11 @@ def tile_grucellmodel_pa_v_kernel(tc, input_seq, W_ih, b_ih, gh, r, z, n, grad_o
                 scales=scales[:],
                 in_=words[s, gate][:].rearrange("p w j -> p (w j)"),
             )
+            quantised[s, gate] = (codes, scales)
+
+        def multiply(s, gate):
+            hq, c = divmod(s, PASSES)
+            codes, scales = quantised[s, gate]
             for half in range(HALVES):
                 if c == 0:
                     acc[gate, half] = psum.tile([M_TILE, I], F32, name="acc", tag="acc")
@@ -242,39 +246,48 @@ def tile_grucellmodel_pa_v_kernel(tc, input_seq, W_ih, b_ih, gh, r, z, n, grad_o
                 nc.sync.dma_start(out=out[row0 : row0 + M_TILE, :], in_=res[:])
 
         nc.vector.memset(minus_half[:], -0.5)
+        nc.scalar.activation(out=warm_up[:], in_=minus_half[:], func=ACT.Square)
         make_identity(nc, identity[:])
+        nc.vector.tensor_scalar_mul(out=minus_identity[:], in0=identity[:], scalar1=-1.0)
         for s in range(LOADS_AHEAD):
             load(s)
+            if 0 <= s - X_LATE < PASSES:
+                load_x(s - X_LATE)
         copy_g(0)
+        copy_into_psum(minus_h_n_psum[:], h_n[:], minus_identity)
         square(0)
-        group_x(0)
         square(1)
 
         LAST = STEPS - 1
+        multiplied = 0
         for s in range(STEPS):
-            hq, c = divmod(s, PASSES)
             if s + LOADS_AHEAD < STEPS:
                 load(s + LOADS_AHEAD)
             multiply_from_psum(s)
             if s > 0:
-                before = s - 1
-                vector_d_r(before, GPSIMD_COLS)
-                if before < PASSES:
-                    quantise_x(before)
+                vector_d_r(s - 1, GPSIMD_COLS)
                 for gate in (D_N, D_R, D_Z):
-                    quantise_and_multiply(before, gate)
-                if c == 0:
+                    quantise(s - 1, gate)
+            x_pass = s - 1 - X_LATE
+            if 0 <= x_pass < PASSES:
+                quantise_x(x_pass)
+            while multiplied < s and (x_pass >= PASSES - 1 or multiplied % PASSES <= x_pass):
+                for gate in (D_N, D_R, D_Z):
+                    multiply(multiplied, gate)
+                if multiplied % PASSES == PASSES - 1:
                     for gate in (D_N, D_R, D_Z):
-                        store(before, gate, False)
+                        store(multiplied, gate, False)
+                multiplied += 1
             finish_d_n(s)
             if s < LAST:
                 gpsimd_share(s)
             if s + SQUARES_AHEAD < STEPS:
                 square(s + SQUARES_AHEAD)
-            if hq == 0 and c + 1 < PASSES:
-                group_x(c + 1)
+            if 0 <= s - 1 < PASSES:
+                group_x(s - 1)
         vector_d_z(LAST)
         vector_d_r(LAST, 0)
         for gate in (D_Z, D_N, D_R):
-            quantise_and_multiply(LAST, gate)
+            quantise(LAST, gate)
+            multiply(LAST, gate)
             store(LAST, gate, gate == D_R)

@@ -23,11 +23,14 @@ H_ROUND = 256
 ROUNDS = H // H_ROUND
 HALVES = H_ROUND // M_TILE
 STEPS = ROUNDS * PASSES
+LAST = STEPS - 1
+ZR = 2 * H_ROUND
 N_MAX = 512
 LOADS_AHEAD = 5
+N_AHEAD = 4
 SQUARES_AHEAD = 2
 X_LATE = 2
-GPSIMD_COLS = 64
+GPSIMD_COLS = 352
 
 FLOPS = 2 * T * B * GATES * H * I
 BYTES = T * B * I * 2 + B * H * 2 + 3 * T * B * H * 4 + B * T * H * 2 + GATES * H * I * 4
@@ -46,12 +49,13 @@ def tile_grucellmodel_pa_v_kernel(tc, input_seq, W_ih, b_ih, gh, r, z, n, grad_o
     with ExitStack() as ctx:
         keep = ctx.enter_context(tc.tile_pool(name="keep", bufs=1))
         loads = ctx.enter_context(tc.tile_pool(name="loads", bufs=LOADS_AHEAD + 1))
+        n_loads = ctx.enter_context(tc.tile_pool(name="n_loads", bufs=N_AHEAD + 1))
         ahead = ctx.enter_context(tc.tile_pool(name="ahead", bufs=SQUARES_AHEAD + 1))
         work = ctx.enter_context(tc.tile_pool(name="work", bufs=2))
         grouped = ctx.enter_context(tc.tile_pool(name="grouped", bufs=2))
         packed = ctx.enter_context(tc.tile_pool(name="packed", bufs=X_LATE + 2))
         results = ctx.enter_context(tc.tile_pool(name="results", bufs=GATES * HALVES))
-        psum = ctx.enter_context(tc.psum_pool(name="psum", bufs=GATES * HALVES))
+        psum = ctx.enter_context(tc.psum_pool(name="psum", bufs=HALVES))
         psum_operands = ctx.enter_context(tc.psum_pool(name="psum_operands", bufs=1))
         ctx.enter_context(tc.manual_schedule())
 
@@ -65,14 +69,16 @@ def tile_grucellmodel_pa_v_kernel(tc, input_seq, W_ih, b_ih, gh, r, z, n, grad_o
         x_codes = keep.tile([P, PASSES, I], U32, align_bytes=64)
         x_scales = keep.tile([P, PASSES, I], U8, align_bytes=64)
         loaded = {}
+        partners = {}
         squared = {}
         x_grouped = {}
         g_psum = {}
+        g_one_minus_z = {}
         factors = {}
-        d_n_of = {}
         words = {}
-        quantised = {}
+        quantised = []
         acc = {}
+        progress = {"multiplied": 0, "x_passes": 0}
 
         def load(s):
             hq, c = divmod(s, PASSES)
@@ -86,23 +92,31 @@ def tile_grucellmodel_pa_v_kernel(tc, input_seq, W_ih, b_ih, gh, r, z, n, grad_o
                 nc.sync.dma_start(out=h_n[:], in_=gh[:, 2 * H : 3 * H])
             r_t = loads.tile([P, PACK, H_ROUND], F32)
             nc.sync.dma_start(out=r_t[:], in_=r[steps, :, h_cols].rearrange("j b h -> b j h"))
-            n_t = loads.tile([P, PACK, H_ROUND], F32)
-            nc.sync.dma_start(out=n_t[:], in_=n[steps, :, h_cols].rearrange("j b h -> b j h"))
-            loaded[s] = (z_t, g_t, n_t, r_t)
+            loaded[s] = (g_t, z_t, r_t)
+
+        def load_n(s):
+            hq, c = divmod(s, PASSES)
+            steps = slice(c * PACK, (c + 1) * PACK)
+            h_cols = slice(hq * H_ROUND, (hq + 1) * H_ROUND)
+            n_dn = n_loads.tile([P, PACK, ZR], F32)
+            nc.sync.dma_start(
+                out=n_dn[:, :, :H_ROUND], in_=n[steps, :, h_cols].rearrange("j b h -> b j h")
+            )
+            partners[s] = n_dn
 
         def load_x(c):
             steps = slice(c * PACK, (c + 1) * PACK)
             nc.sync.dma_start(out=x_rows[:, c, :, :], in_=input_seq[steps].rearrange("j b i -> b j i"))
 
         def square(s):
-            z_t, g_t, n_t, r_t = loaded[s]
+            g_t, z_t, r_t = loaded[s]
             zc2 = ahead.tile([P, PACK, H_ROUND], F32)
             nc.scalar.activation(out=zc2[:], in_=z_t[:], func=ACT.Square, bias=minus_half[:])
             rc2 = ahead.tile([P, PACK, H_ROUND], F32)
             nc.scalar.activation(out=rc2[:], in_=r_t[:], func=ACT.Square, bias=minus_half[:])
             nn = ahead.tile([P, PACK, H_ROUND], F32)
-            nc.scalar.activation(out=nn[:], in_=n_t[:], func=ACT.Square)
-            squared[s] = (nn, zc2, rc2)
+            nc.scalar.activation(out=nn[:], in_=partners[s][:, :, :H_ROUND], func=ACT.Square)
+            squared[s] = (zc2, rc2, nn)
 
         def copy_into_psum(dst, src, diagonal):
             for col0 in range(0, dst.shape[1], N_MAX):
@@ -115,7 +129,7 @@ def tile_grucellmodel_pa_v_kernel(tc, input_seq, W_ih, b_ih, gh, r, z, n, grad_o
                 )
 
         def copy_g(s):
-            z_t, g_t, n_t, r_t = loaded[s]
+            g_t, z_t, r_t = loaded[s]
             g_p = psum_operands.tile([P, PACK * H_ROUND], BF16)
             copy_into_psum(g_p[:], g_t[:].rearrange("p j h -> p (j h)"), identity)
             g_psum[s] = g_p
@@ -128,75 +142,51 @@ def tile_grucellmodel_pa_v_kernel(tc, input_seq, W_ih, b_ih, gh, r, z, n, grad_o
         def multiply_from_psum(s):
             hq, c = divmod(s, PASSES)
             h_cols = slice(hq * H_ROUND, (hq + 1) * H_ROUND)
-            nn, zc2, rc2 = squared[s]
+            g_t, z_t, r_t = loaded[s]
+            zc2, rc2, nn = squared[s]
             g_rows = g_psum[s][:].rearrange("p (j h) -> p j h", j=PACK)
-            gn = work.tile([P, PACK, H_ROUND], F32)
+            gw = work.tile([P, PACK, H_ROUND], F32)
             nc.vector.scalar_tensor_tensor(
-                out=gn[:], in0=loaded[s][0][:], scalar=1.0, in1=g_rows, op0=ALU.subtract, op1=ALU.mult
+                out=gw[:], in0=z_t[:], scalar=1.0, in1=g_rows, op0=ALU.subtract, op1=ALU.mult
             )
-            gz = work.tile([P, PACK, H_ROUND], F32)
+            g_one_minus_z[s] = gw
+            gz_rh = work.tile([P, PACK, ZR], F32)
             nc.vector.scalar_tensor_tensor(
-                out=gz[:], in0=zc2[:], scalar=0.25, in1=g_rows, op0=ALU.subtract, op1=ALU.mult
+                out=gz_rh[:, :, :H_ROUND],
+                in0=zc2[:],
+                scalar=0.25,
+                in1=g_rows,
+                op0=ALU.subtract,
+                op1=ALU.mult,
             )
             if s + 1 < STEPS:
                 copy_g(s + 1)
-            rh = work.tile([P, PACK, H_ROUND], F32)
             nc.vector.scalar_tensor_tensor(
-                out=rh[:],
+                out=gz_rh[:, :, H_ROUND:],
                 in0=rc2[:],
                 scalar=0.25,
                 in1=minus_h_n_psum[:, h_cols].unsqueeze(1).to_broadcast([P, PACK, H_ROUND]),
                 op0=ALU.subtract,
                 op1=ALU.mult,
             )
-            factors[s] = (gn, gz, rh)
+            factors[s] = gz_rh
 
         def finish_d_n(s):
-            nn, zc2, rc2 = squared[s]
-            gn, gz, rh = factors[s]
-            d_n = work.tile([P, PACK, H_ROUND], F32)
+            zc2, rc2, nn = squared[s]
+            d_n = partners[s][:, :, H_ROUND:]
             nc.vector.scalar_tensor_tensor(
-                out=d_n[:], in0=nn[:], scalar=1.0, in1=gn[:], op0=ALU.subtract, op1=ALU.mult
+                out=d_n, in0=nn[:], scalar=1.0, in1=g_one_minus_z[s][:], op0=ALU.subtract, op1=ALU.mult
             )
-            d_n_of[s] = d_n
             dn_words = grouped.tile([P, H_ROUND, PACK], BF16, align_bytes=64)
-            nc.scalar.copy(out=words_in_fours(dn_words[:]), in_=rows_in_fours(d_n[:]))
+            nc.scalar.copy(out=words_in_fours(dn_words[:]), in_=rows_in_fours(d_n))
             words[s, D_N] = dn_words
-            words[s, D_R] = grouped.tile([P, H_ROUND, PACK], BF16, align_bytes=64, name="dr_words")
-            words[s, D_Z] = grouped.tile([P, H_ROUND, PACK], BF16, align_bytes=64, name="dz_words")
+            words[s, D_Z] = grouped.tile([P, ZR, PACK], BF16, align_bytes=64, name="zr_words")
 
-        def gpsimd_share(s):
-            z_t, g_t, n_t, r_t = loaded[s]
-            gn, gz, rh = factors[s]
-            nc.gpsimd.tensor_tensor(
-                out=words_in_fours(words[s, D_R][:, :GPSIMD_COLS, :]),
-                in0=rows_in_fours(rh[:, :, :GPSIMD_COLS]),
-                in1=rows_in_fours(d_n_of[s][:, :, :GPSIMD_COLS]),
-                op=ALU.mult,
-            )
-            nc.gpsimd.tensor_tensor(
-                out=words_in_fours(words[s, D_Z][:]),
-                in0=rows_in_fours(gz[:]),
-                in1=rows_in_fours(n_t[:]),
-                op=ALU.mult,
-            )
-
-        def vector_d_r(s, col0):
-            gn, gz, rh = factors[s]
-            nc.vector.tensor_tensor(
-                out=words_in_fours(words[s, D_R][:, col0:, :]),
-                in0=rows_in_fours(rh[:, :, col0:]),
-                in1=rows_in_fours(d_n_of[s][:, :, col0:]),
-                op=ALU.mult,
-            )
-
-        def vector_d_z(s):
-            z_t, g_t, n_t, r_t = loaded[s]
-            gn, gz, rh = factors[s]
-            nc.vector.tensor_tensor(
-                out=words_in_fours(words[s, D_Z][:]),
-                in0=rows_in_fours(gz[:]),
-                in1=rows_in_fours(n_t[:]),
+        def finish_d_z_d_r(engine, s, col0, col1):
+            engine.tensor_tensor(
+                out=words_in_fours(words[s, D_Z][:, col0:col1, :]),
+                in0=rows_in_fours(factors[s][:, :, col0:col1]),
+                in1=rows_in_fours(partners[s][:, :, col0:col1]),
                 op=ALU.mult,
             )
 
@@ -206,44 +196,51 @@ def tile_grucellmodel_pa_v_kernel(tc, input_seq, W_ih, b_ih, gh, r, z, n, grad_o
                 scales=x_scales[:, c, :],
                 in_=x_grouped[c][:].rearrange("p w j -> p (w j)"),
             )
+            progress["x_passes"] = c + 1
 
-        def quantise(s, gate):
-            codes = packed.tile([P, H_ROUND], U32, align_bytes=64, name="codes", tag="codes%d" % gate)
-            scales = packed.tile([P, H_ROUND], U8, align_bytes=64, name="scales", tag="scales%d" % gate)
+        def quantise(s, *gates):
+            width = len(gates) * H_ROUND
+            codes = packed.tile([P, width], U32, align_bytes=64, name="codes", tag="codes%d" % gates[0])
+            scales = packed.tile([P, width], U8, align_bytes=64, name="scales", tag="scales%d" % gates[0])
             nc.vector.quantize_mx(
                 out=codes[:].bitcast(E5M2_X4),
                 scales=scales[:],
-                in_=words[s, gate][:].rearrange("p w j -> p (w j)"),
+                in_=words[s, gates[0]][:].rearrange("p w j -> p (w j)"),
             )
-            quantised[s, gate] = (codes, scales)
+            quantised.append((s, gates, codes, scales))
 
-        def multiply(s, gate):
-            hq, c = divmod(s, PASSES)
-            codes, scales = quantised[s, gate]
-            for half in range(HALVES):
-                if c == 0:
-                    acc[gate, half] = psum.tile([M_TILE, I], F32, name="acc", tag="acc")
-                m_cols = slice(half * M_TILE, (half + 1) * M_TILE)
-                nc.tensor.matmul_mx(
-                    out=acc[gate, half][:],
-                    lhsT=codes[:, m_cols].bitcast(E5M2_X4),
-                    lhsT_scale=scales[:, m_cols],
-                    rhs=x_codes[:, c, :].bitcast(E4M3_X4),
-                    rhs_scale=x_scales[:, c, :],
-                    start=(c == 0),
-                    stop=(c == PASSES - 1),
-                )
-
-        def store(s, gate, on_vector):
-            hq, c = divmod(s, PASSES)
-            for half in range(HALVES):
-                row0 = gate * H + hq * H_ROUND + half * M_TILE
-                res = results.tile([M_TILE, I], F32)
-                if on_vector and half == HALVES - 1:
-                    nc.vector.tensor_copy(out=res[:], in_=acc[gate, half][:])
-                else:
-                    nc.scalar.copy(out=res[:], in_=acc[gate, half][:])
-                nc.sync.dma_start(out=out[row0 : row0 + M_TILE, :], in_=res[:])
+        def multiply_what_is_ready(last_on_vector):
+            while progress["multiplied"] < len(quantised):
+                s, gates, codes, scales = quantised[progress["multiplied"]]
+                hq, c = divmod(s, PASSES)
+                if c >= progress["x_passes"]:
+                    break
+                progress["multiplied"] += 1
+                for place, gate in enumerate(gates):
+                    for half in range(HALVES):
+                        if c == 0:
+                            acc[gate, half] = psum.tile([M_TILE, I], F32, name="acc", tag="acc%d" % gate)
+                        col0 = place * H_ROUND + half * M_TILE
+                        nc.tensor.matmul_mx(
+                            out=acc[gate, half][:],
+                            lhsT=codes[:, col0 : col0 + M_TILE].bitcast(E5M2_X4),
+                            lhsT_scale=scales[:, col0 : col0 + M_TILE],
+                            rhs=x_codes[:, c, :].bitcast(E4M3_X4),
+                            rhs_scale=x_scales[:, c, :],
+                            start=(c == 0),
+                            stop=(c == PASSES - 1),
+                        )
+                if c < PASSES - 1:
+                    continue
+                for gate in gates:
+                    for half in range(HALVES):
+                        row0 = gate * H + hq * H_ROUND + half * M_TILE
+                        res = results.tile([M_TILE, I], F32)
+                        if last_on_vector and gate == gates[-1] and half == HALVES - 1:
+                            nc.vector.tensor_copy(out=res[:], in_=acc[gate, half][:])
+                        else:
+                            nc.scalar.copy(out=res[:], in_=acc[gate, half][:])
+                        nc.sync.dma_start(out=out[row0 : row0 + M_TILE, :], in_=res[:])
 
         nc.vector.memset(minus_half[:], -0.5)
         nc.scalar.activation(out=warm_up[:], in_=minus_half[:], func=ACT.Square)
@@ -251,6 +248,8 @@ def tile_grucellmodel_pa_v_kernel(tc, input_seq, W_ih, b_ih, gh, r, z, n, grad_o
         nc.vector.tensor_scalar_mul(out=minus_identity[:], in0=identity[:], scalar1=-1.0)
         for s in range(LOADS_AHEAD):
             load(s)
+            if s < N_AHEAD:
+                load_n(s)
             if 0 <= s - X_LATE < PASSES:
                 load_x(s - X_LATE)
         copy_g(0)
@@ -258,36 +257,30 @@ def tile_grucellmodel_pa_v_kernel(tc, input_seq, W_ih, b_ih, gh, r, z, n, grad_o
         square(0)
         square(1)
 
-        LAST = STEPS - 1
-        multiplied = 0
         for s in range(STEPS):
             if s + LOADS_AHEAD < STEPS:
                 load(s + LOADS_AHEAD)
             multiply_from_psum(s)
-            if s > 0:
-                vector_d_r(s - 1, GPSIMD_COLS)
-                for gate in (D_N, D_R, D_Z):
-                    quantise(s - 1, gate)
-            x_pass = s - 1 - X_LATE
-            if 0 <= x_pass < PASSES:
-                quantise_x(x_pass)
-            while multiplied < s and (x_pass >= PASSES - 1 or multiplied % PASSES <= x_pass):
-                for gate in (D_N, D_R, D_Z):
-                    multiply(multiplied, gate)
-                if multiplied % PASSES == PASSES - 1:
-                    for gate in (D_N, D_R, D_Z):
-                        store(multiplied, gate, False)
-                multiplied += 1
+            if s >= 2:
+                quantise(s - 2, D_Z, D_R)
+            if s >= 1:
+                finish_d_z_d_r(nc.vector, s - 1, GPSIMD_COLS, ZR)
+                quantise(s - 1, D_N)
+            if s + N_AHEAD < STEPS:
+                load_n(s + N_AHEAD)
+            if 0 <= s - 1 - X_LATE < PASSES:
+                quantise_x(s - 1 - X_LATE)
+            multiply_what_is_ready(False)
             finish_d_n(s)
             if s < LAST:
-                gpsimd_share(s)
+                finish_d_z_d_r(nc.gpsimd, s, 0, GPSIMD_COLS)
             if s + SQUARES_AHEAD < STEPS:
                 square(s + SQUARES_AHEAD)
             if 0 <= s - 1 < PASSES:
                 group_x(s - 1)
-        vector_d_z(LAST)
-        vector_d_r(LAST, 0)
-        for gate in (D_Z, D_N, D_R):
-            quantise(LAST, gate)
-            multiply(LAST, gate)
-            store(LAST, gate, gate == D_R)
+        quantise(LAST - 1, D_Z, D_R)
+        finish_d_z_d_r(nc.vector, LAST, 0, ZR)
+        quantise(LAST, D_N)
+        multiply_what_is_ready(False)
+        quantise(LAST, D_Z, D_R)
+        multiply_what_is_ready(True)

@@ -30,7 +30,7 @@ LOADS_AHEAD = 5
 N_AHEAD = 4
 SQUARES_AHEAD = 2
 X_LATE = 2
-GPSIMD_COLS = 352
+GPSIMD_COLS = 384
 
 FLOPS = 2 * T * B * GATES * H * I
 BYTES = T * B * I * 2 + B * H * 2 + 3 * T * B * H * 4 + B * T * H * 2 + GATES * H * I * 4

@@ -265,15 +265,16 @@ def tile_grucellmodel_pa_v_kernel(tc, input_seq, W_ih, b_ih, gh, r, z, n, grad_o
                 quantise(s - 2, D_Z, D_R)
             if s >= 1:
                 finish_d_z_d_r(nc.vector, s - 1, GPSIMD_COLS, ZR)
-                quantise(s - 1, D_N)
             if s + N_AHEAD < STEPS:
                 load_n(s + N_AHEAD)
             if 0 <= s - 1 - X_LATE < PASSES:
                 quantise_x(s - 1 - X_LATE)
-            multiply_what_is_ready(False)
             finish_d_n(s)
             if s < LAST:
                 finish_d_z_d_r(nc.gpsimd, s, 0, GPSIMD_COLS)
+            if s >= 1:
+                quantise(s - 1, D_N)
+            multiply_what_is_ready(False)
             if s + SQUARES_AHEAD < STEPS:
                 square(s + SQUARES_AHEAD)
             if 0 <= s - 1 < PASSES:

@@ -27,10 +27,10 @@ LAST = STEPS - 1
 ZR = 2 * H_ROUND
 N_MAX = 512
 LOADS_AHEAD = 5
-N_AHEAD = 4
 SQUARES_AHEAD = 2
 X_LATE = 2
 GPSIMD_COLS = 384
+FIRST_PIECES = (slice(0, 2), slice(2, 4))
 
 FLOPS = 2 * T * B * GATES * H * I
 BYTES = T * B * I * 2 + B * H * 2 + 3 * T * B * H * 4 + B * T * H * 2 + GATES * H * I * 4
@@ -49,8 +49,6 @@ def tile_grucellmodel_pa_v_kernel(tc, input_seq, W_ih, b_ih, gh, r, z, n, grad_o
     with ExitStack() as ctx:
         keep = ctx.enter_context(tc.tile_pool(name="keep", bufs=1))
         loads = ctx.enter_context(tc.tile_pool(name="loads", bufs=LOADS_AHEAD + 1))
-        n_loads = ctx.enter_context(tc.tile_pool(name="n_loads", bufs=N_AHEAD + 1))
-        ahead = ctx.enter_context(tc.tile_pool(name="ahead", bufs=SQUARES_AHEAD + 1))
         work = ctx.enter_context(tc.tile_pool(name="work", bufs=2))
         grouped = ctx.enter_context(tc.tile_pool(name="grouped", bufs=2))
         packed = ctx.enter_context(tc.tile_pool(name="packed", bufs=X_LATE + 2))
@@ -69,69 +67,87 @@ def tile_grucellmodel_pa_v_kernel(tc, input_seq, W_ih, b_ih, gh, r, z, n, grad_o
         x_codes = keep.tile([P, PASSES, I], U32, align_bytes=64)
         x_scales = keep.tile([P, PASSES, I], U8, align_bytes=64)
         loaded = {}
+        factors = {}
         partners = {}
-        squared = {}
         x_grouped = {}
         g_psum = {}
         g_one_minus_z = {}
-        factors = {}
-        words = {}
+        dn_words = {}
+        zr_words = {}
         quantised = []
         acc = {}
-        progress = {"multiplied": 0, "x_passes": 0}
+        occupied = []
+        complete = []
+        progress = {"x_passes": 0}
+
+        def place(s):
+            hq, c = divmod(s, PASSES)
+            return slice(c * PACK, (c + 1) * PACK), slice(hq * H_ROUND, (hq + 1) * H_ROUND)
+
+        def pieces(s):
+            return FIRST_PIECES if s == 0 else (slice(0, PACK),)
+
+        def at(s, js):
+            step0 = (s % PASSES) * PACK
+            return slice(step0 + js.start, step0 + js.stop)
+
+        def load_h_n(col0, col1):
+            nc.sync.dma_start(out=h_n[:, col0:col1], in_=gh[:, 2 * H + col0 : 2 * H + col1])
 
         def load(s):
-            hq, c = divmod(s, PASSES)
-            steps = slice(c * PACK, (c + 1) * PACK)
-            h_cols = slice(hq * H_ROUND, (hq + 1) * H_ROUND)
+            steps, h_cols = place(s)
             g_t = loads.tile([P, PACK, H_ROUND], BF16)
             nc.sync.dma_start(out=g_t[:], in_=grad_out[:, steps, h_cols])
             z_t = loads.tile([P, PACK, H_ROUND], F32)
-            nc.sync.dma_start(out=z_t[:], in_=z[steps, :, h_cols].rearrange("j b h -> b j h"))
+            for js in pieces(s):
+                nc.sync.dma_start(out=z_t[:, js, :], in_=z[at(s, js), :, h_cols].rearrange("j b h -> b j h"))
             if s == 0:
-                nc.sync.dma_start(out=h_n[:], in_=gh[:, 2 * H : 3 * H])
-            r_t = loads.tile([P, PACK, H_ROUND], F32)
-            nc.sync.dma_start(out=r_t[:], in_=r[steps, :, h_cols].rearrange("j b h -> b j h"))
-            loaded[s] = (g_t, z_t, r_t)
-
-        def load_n(s):
-            hq, c = divmod(s, PASSES)
-            steps = slice(c * PACK, (c + 1) * PACK)
-            h_cols = slice(hq * H_ROUND, (hq + 1) * H_ROUND)
-            n_dn = n_loads.tile([P, PACK, ZR], F32)
-            nc.sync.dma_start(
-                out=n_dn[:, :, :H_ROUND], in_=n[steps, :, h_cols].rearrange("j b h -> b j h")
-            )
+                load_h_n(0, H_ROUND)
+            gz_rh = loads.tile([P, PACK, ZR], F32)
+            for js in pieces(s):
+                nc.sync.dma_start(out=gz_rh[:, js, H_ROUND:], in_=r[at(s, js), :, h_cols].rearrange("j b h -> b j h"))
+            n_dn = loads.tile([P, PACK, ZR], F32)
+            for js in pieces(s):
+                nc.sync.dma_start(out=n_dn[:, js, :H_ROUND], in_=n[at(s, js), :, h_cols].rearrange("j b h -> b j h"))
+            loaded[s] = (g_t, z_t)
+            factors[s] = gz_rh
             partners[s] = n_dn
 
         def load_x(c):
             steps = slice(c * PACK, (c + 1) * PACK)
             nc.sync.dma_start(out=x_rows[:, c, :, :], in_=input_seq[steps].rearrange("j b i -> b j i"))
 
-        def square(s):
-            g_t, z_t, r_t = loaded[s]
-            zc2 = ahead.tile([P, PACK, H_ROUND], F32)
-            nc.scalar.activation(out=zc2[:], in_=z_t[:], func=ACT.Square, bias=minus_half[:])
-            rc2 = ahead.tile([P, PACK, H_ROUND], F32)
-            nc.scalar.activation(out=rc2[:], in_=r_t[:], func=ACT.Square, bias=minus_half[:])
-            nn = ahead.tile([P, PACK, H_ROUND], F32)
-            nc.scalar.activation(out=nn[:], in_=partners[s][:, :, :H_ROUND], func=ACT.Square)
-            squared[s] = (zc2, rc2, nn)
+        def square_z_r(s):
+            z_t = loaded[s][1]
+            gz_rh = factors[s]
+            for js in pieces(s):
+                nc.scalar.activation(
+                    out=gz_rh[:, js, :H_ROUND], in_=z_t[:, js, :], func=ACT.Square, bias=minus_half[:]
+                )
+            for js in pieces(s):
+                rh = gz_rh[:, js, H_ROUND:]
+                nc.scalar.activation(out=rh, in_=rh, func=ACT.Square, bias=minus_half[:])
+
+        def square_n(s):
+            n_dn = partners[s]
+            for js in pieces(s):
+                nc.scalar.activation(out=n_dn[:, js, H_ROUND:], in_=n_dn[:, js, :H_ROUND], func=ACT.Square)
 
         def copy_into_psum(dst, src, diagonal):
-            for col0 in range(0, dst.shape[1], N_MAX):
+            width = dst.shape[1]
+            for col0 in range(0, width, N_MAX):
+                cols = slice(col0, min(col0 + N_MAX, width))
                 nc.tensor.matmul(
-                    out=dst[:, col0 : col0 + N_MAX],
+                    out=dst[:, cols],
                     lhsT=diagonal[:],
-                    rhs=src[:, col0 : col0 + N_MAX],
+                    rhs=src[:, cols],
                     start=True,
                     stop=True,
                 )
 
         def copy_g(s):
-            g_t, z_t, r_t = loaded[s]
             g_p = psum_operands.tile([P, PACK * H_ROUND], BF16)
-            copy_into_psum(g_p[:], g_t[:].rearrange("p j h -> p (j h)"), identity)
+            copy_into_psum(g_p[:], loaded[s][0][:].rearrange("p j h -> p (j h)"), identity)
             g_psum[s] = g_p
 
         def group_x(c):
@@ -140,51 +156,61 @@ def tile_grucellmodel_pa_v_kernel(tc, input_seq, W_ih, b_ih, gh, r, z, n, grad_o
             x_grouped[c] = x_words
 
         def multiply_from_psum(s):
-            hq, c = divmod(s, PASSES)
-            h_cols = slice(hq * H_ROUND, (hq + 1) * H_ROUND)
-            g_t, z_t, r_t = loaded[s]
-            zc2, rc2, nn = squared[s]
+            h_cols = place(s)[1]
+            z_t = loaded[s][1]
+            gz = factors[s][:, :, :H_ROUND]
+            rh = factors[s][:, :, H_ROUND:]
             g_rows = g_psum[s][:].rearrange("p (j h) -> p j h", j=PACK)
             gw = work.tile([P, PACK, H_ROUND], F32)
-            nc.vector.scalar_tensor_tensor(
-                out=gw[:], in0=z_t[:], scalar=1.0, in1=g_rows, op0=ALU.subtract, op1=ALU.mult
-            )
+            for js in pieces(s):
+                nc.vector.scalar_tensor_tensor(
+                    out=gw[:, js, :],
+                    in0=z_t[:, js, :],
+                    scalar=1.0,
+                    in1=g_rows[:, js, :],
+                    op0=ALU.subtract,
+                    op1=ALU.mult,
+                )
             g_one_minus_z[s] = gw
-            gz_rh = work.tile([P, PACK, ZR], F32)
-            nc.vector.scalar_tensor_tensor(
-                out=gz_rh[:, :, :H_ROUND],
-                in0=zc2[:],
-                scalar=0.25,
-                in1=g_rows,
-                op0=ALU.subtract,
-                op1=ALU.mult,
-            )
-            if s + 1 < STEPS:
+            for js in pieces(s):
+                nc.vector.scalar_tensor_tensor(
+                    out=gz[:, js, :],
+                    in0=gz[:, js, :],
+                    scalar=0.25,
+                    in1=g_rows[:, js, :],
+                    op0=ALU.subtract,
+                    op1=ALU.mult,
+                )
+            if s < LAST:
                 copy_g(s + 1)
-            nc.vector.scalar_tensor_tensor(
-                out=gz_rh[:, :, H_ROUND:],
-                in0=rc2[:],
-                scalar=0.25,
-                in1=minus_h_n_psum[:, h_cols].unsqueeze(1).to_broadcast([P, PACK, H_ROUND]),
-                op0=ALU.subtract,
-                op1=ALU.mult,
-            )
-            factors[s] = gz_rh
+            for js in pieces(s):
+                nc.vector.scalar_tensor_tensor(
+                    out=rh[:, js, :],
+                    in0=rh[:, js, :],
+                    scalar=0.25,
+                    in1=minus_h_n_psum[:, h_cols].unsqueeze(1).to_broadcast([P, js.stop - js.start, H_ROUND]),
+                    op0=ALU.subtract,
+                    op1=ALU.mult,
+                )
 
         def finish_d_n(s):
-            zc2, rc2, nn = squared[s]
             d_n = partners[s][:, :, H_ROUND:]
-            nc.vector.scalar_tensor_tensor(
-                out=d_n, in0=nn[:], scalar=1.0, in1=g_one_minus_z[s][:], op0=ALU.subtract, op1=ALU.mult
-            )
-            dn_words = grouped.tile([P, H_ROUND, PACK], BF16, align_bytes=64)
-            nc.scalar.copy(out=words_in_fours(dn_words[:]), in_=rows_in_fours(d_n))
-            words[s, D_N] = dn_words
-            words[s, D_Z] = grouped.tile([P, ZR, PACK], BF16, align_bytes=64, name="zr_words")
+            for js in pieces(s):
+                nc.vector.scalar_tensor_tensor(
+                    out=d_n[:, js, :],
+                    in0=d_n[:, js, :],
+                    scalar=1.0,
+                    in1=g_one_minus_z[s][:, js, :],
+                    op0=ALU.subtract,
+                    op1=ALU.mult,
+                )
+            dn_words[s] = grouped.tile([P, H_ROUND, PACK], BF16, align_bytes=64, name="dn_words")
+            nc.scalar.copy(out=words_in_fours(dn_words[s][:]), in_=rows_in_fours(d_n))
+            zr_words[s] = grouped.tile([P, ZR, PACK], BF16, align_bytes=64, name="zr_words")
 
         def finish_d_z_d_r(engine, s, col0, col1):
             engine.tensor_tensor(
-                out=words_in_fours(words[s, D_Z][:, col0:col1, :]),
+                out=words_in_fours(zr_words[s][:, col0:col1, :]),
                 in0=rows_in_fours(factors[s][:, :, col0:col1]),
                 in1=rows_in_fours(partners[s][:, :, col0:col1]),
                 op=ALU.mult,
@@ -198,49 +224,65 @@ def tile_grucellmodel_pa_v_kernel(tc, input_seq, W_ih, b_ih, gh, r, z, n, grad_o
             )
             progress["x_passes"] = c + 1
 
-        def quantise(s, *gates):
-            width = len(gates) * H_ROUND
-            codes = packed.tile([P, width], U32, align_bytes=64, name="codes", tag="codes%d" % gates[0])
-            scales = packed.tile([P, width], U8, align_bytes=64, name="scales", tag="scales%d" % gates[0])
+        def quantise(s, source, tiles, tag):
+            width = len(tiles) * M_TILE
+            codes = packed.tile([P, width], U32, align_bytes=64, name="codes", tag="codes_" + tag)
+            scales = packed.tile([P, width], U8, align_bytes=64, name="scales", tag="scales_" + tag)
             nc.vector.quantize_mx(
                 out=codes[:].bitcast(E5M2_X4),
                 scales=scales[:],
-                in_=words[s, gates[0]][:].rearrange("p w j -> p (w j)"),
+                in_=source.rearrange("p w j -> p (w j)"),
             )
-            quantised.append((s, gates, codes, scales))
+            quantised.append((s, tiles, codes, scales))
 
-        def multiply_what_is_ready(last_on_vector):
-            while progress["multiplied"] < len(quantised):
-                s, gates, codes, scales = quantised[progress["multiplied"]]
+        def quantise_d_n(s):
+            quantise(s, dn_words[s][:], [(D_N, half) for half in range(HALVES)], "n")
+
+        def quantise_d_z_d_r(s, first_tile, last_tile):
+            tiles = [(gate, half) for gate in (D_Z, D_R) for half in range(HALVES)]
+            quantise(
+                s,
+                zr_words[s][:, first_tile * M_TILE : last_tile * M_TILE, :],
+                tiles[first_tile:last_tile],
+                "zr",
+            )
+
+        def multiply_what_is_ready():
+            for entry in list(quantised):
+                s, tiles, codes, scales = entry
                 hq, c = divmod(s, PASSES)
-                if c >= progress["x_passes"]:
-                    break
-                progress["multiplied"] += 1
-                for place, gate in enumerate(gates):
-                    for half in range(HALVES):
-                        if c == 0:
-                            acc[gate, half] = psum.tile([M_TILE, I], F32, name="acc", tag="acc%d" % gate)
-                        col0 = place * H_ROUND + half * M_TILE
-                        nc.tensor.matmul_mx(
-                            out=acc[gate, half][:],
-                            lhsT=codes[:, col0 : col0 + M_TILE].bitcast(E5M2_X4),
-                            lhsT_scale=scales[:, col0 : col0 + M_TILE],
-                            rhs=x_codes[:, c, :].bitcast(E4M3_X4),
-                            rhs_scale=x_scales[:, c, :],
-                            start=(c == 0),
-                            stop=(c == PASSES - 1),
-                        )
-                if c < PASSES - 1:
+                if c >= progress["x_passes"] or (c == 0 and any(t in occupied for t in tiles)):
                     continue
-                for gate in gates:
-                    for half in range(HALVES):
-                        row0 = gate * H + hq * H_ROUND + half * M_TILE
-                        res = results.tile([M_TILE, I], F32)
-                        if last_on_vector and gate == gates[-1] and half == HALVES - 1:
-                            nc.vector.tensor_copy(out=res[:], in_=acc[gate, half][:])
-                        else:
-                            nc.scalar.copy(out=res[:], in_=acc[gate, half][:])
-                        nc.sync.dma_start(out=out[row0 : row0 + M_TILE, :], in_=res[:])
+                if c > 0 and any(e[0] < s and e[1][0] == tiles[0] for e in quantised):
+                    continue
+                quantised.remove(entry)
+                for k, (gate, half) in enumerate(tiles):
+                    if c == 0:
+                        acc[gate, half] = psum.tile([M_TILE, I], F32, name="acc", tag="acc%d" % gate)
+                        occupied.append((gate, half))
+                    cols = slice(k * M_TILE, (k + 1) * M_TILE)
+                    nc.tensor.matmul_mx(
+                        out=acc[gate, half][:],
+                        lhsT=codes[:, cols].bitcast(E5M2_X4),
+                        lhsT_scale=scales[:, cols],
+                        rhs=x_codes[:, c, :].bitcast(E4M3_X4),
+                        rhs_scale=x_scales[:, c, :],
+                        start=(c == 0),
+                        stop=(c == PASSES - 1),
+                    )
+                    if c == PASSES - 1:
+                        complete.append((hq, gate, half))
+
+        def empty_psum(copy, count, parts=1):
+            for hq, gate, half in complete[:count]:
+                row0 = gate * H + hq * H_ROUND + half * M_TILE
+                res = results.tile([M_TILE, I], F32)
+                for part in range(parts):
+                    cols = slice(part * I // parts, (part + 1) * I // parts)
+                    copy(out=res[:, cols], in_=acc[gate, half][:, cols])
+                    nc.sync.dma_start(out=out[row0 : row0 + M_TILE, cols], in_=res[:, cols])
+                occupied.remove((gate, half))
+                complete.remove((hq, gate, half))
 
         nc.vector.memset(minus_half[:], -0.5)
         nc.scalar.activation(out=warm_up[:], in_=minus_half[:], func=ACT.Square)
@@ -248,40 +290,52 @@ def tile_grucellmodel_pa_v_kernel(tc, input_seq, W_ih, b_ih, gh, r, z, n, grad_o
         nc.vector.tensor_scalar_mul(out=minus_identity[:], in0=identity[:], scalar1=-1.0)
         for s in range(LOADS_AHEAD):
             load(s)
-            if s < N_AHEAD:
-                load_n(s)
+            if s == 1:
+                load_h_n(H_ROUND, H)
             if 0 <= s - X_LATE < PASSES:
                 load_x(s - X_LATE)
         copy_g(0)
-        copy_into_psum(minus_h_n_psum[:], h_n[:], minus_identity)
-        square(0)
-        square(1)
+        copy_into_psum(minus_h_n_psum[:, :H_ROUND], h_n[:, :H_ROUND], minus_identity)
+        square_z_r(0)
+        square_n(0)
+        square_z_r(1)
 
         for s in range(STEPS):
-            if s + LOADS_AHEAD < STEPS:
-                load(s + LOADS_AHEAD)
             multiply_from_psum(s)
-            if s >= 2:
-                quantise(s - 2, D_Z, D_R)
+            if s == 0:
+                copy_into_psum(minus_h_n_psum[:, H_ROUND:], h_n[:, H_ROUND:], minus_identity)
             if s >= 1:
                 finish_d_z_d_r(nc.vector, s - 1, GPSIMD_COLS, ZR)
-            if s + N_AHEAD < STEPS:
-                load_n(s + N_AHEAD)
+                quantise_d_n(s - 1)
+            if s + LOADS_AHEAD < STEPS:
+                load(s + LOADS_AHEAD)
             if 0 <= s - 1 - X_LATE < PASSES:
                 quantise_x(s - 1 - X_LATE)
             finish_d_n(s)
             if s < LAST:
                 finish_d_z_d_r(nc.gpsimd, s, 0, GPSIMD_COLS)
             if s >= 1:
-                quantise(s - 1, D_N)
-            multiply_what_is_ready(False)
+                quantise_d_z_d_r(s - 1, 0, 4)
+            if s < LAST:
+                square_n(s + 1)
             if s + SQUARES_AHEAD < STEPS:
-                square(s + SQUARES_AHEAD)
+                square_z_r(s + SQUARES_AHEAD)
+            multiply_what_is_ready()
+            empty_psum(nc.scalar.copy, 4)
             if 0 <= s - 1 < PASSES:
                 group_x(s - 1)
-        quantise(LAST - 1, D_Z, D_R)
-        finish_d_z_d_r(nc.vector, LAST, 0, ZR)
-        quantise(LAST, D_N)
-        multiply_what_is_ready(False)
-        quantise(LAST, D_Z, D_R)
-        multiply_what_is_ready(True)
+        finish_d_z_d_r(nc.vector, LAST, 0, H_ROUND)
+        quantise_d_n(LAST)
+        multiply_what_is_ready()
+        empty_psum(nc.scalar.copy, 2)
+        finish_d_z_d_r(nc.vector, LAST, H_ROUND, ZR - M_TILE)
+        quantise_d_z_d_r(LAST, 0, 2)
+        multiply_what_is_ready()
+        finish_d_z_d_r(nc.vector, LAST, ZR - M_TILE, ZR)
+        empty_psum(nc.scalar.copy, 2)
+        quantise_d_z_d_r(LAST, 2, 3)
+        multiply_what_is_ready()
+        quantise_d_z_d_r(LAST, 3, 4)
+        multiply_what_is_ready()
+        empty_psum(nc.vector.tensor_copy, 1, parts=2)
+        empty_psum(nc.scalar.copy, 1, parts=2)

@@ -49,6 +49,7 @@ def tile_grucellmodel_pa_v_kernel(tc, input_seq, W_ih, b_ih, gh, r, z, n, grad_o
     with ExitStack() as ctx:
         keep = ctx.enter_context(tc.tile_pool(name="keep", bufs=1))
         loads = ctx.enter_context(tc.tile_pool(name="loads", bufs=LOADS_AHEAD + 1))
+        ahead = ctx.enter_context(tc.tile_pool(name="ahead", bufs=SQUARES_AHEAD + 2))
         work = ctx.enter_context(tc.tile_pool(name="work", bufs=2))
         grouped = ctx.enter_context(tc.tile_pool(name="grouped", bufs=2))
         packed = ctx.enter_context(tc.tile_pool(name="packed", bufs=X_LATE + 2))
@@ -98,19 +99,18 @@ def tile_grucellmodel_pa_v_kernel(tc, input_seq, W_ih, b_ih, gh, r, z, n, grad_o
             steps, h_cols = place(s)
             g_t = loads.tile([P, PACK, H_ROUND], BF16)
             nc.sync.dma_start(out=g_t[:], in_=grad_out[:, steps, h_cols])
-            z_t = loads.tile([P, PACK, H_ROUND], F32)
+            z_r = loads.tile([P, PACK, ZR], F32)
+            z_t = z_r[:, :, :H_ROUND]
             for js in pieces(s):
                 nc.sync.dma_start(out=z_t[:, js, :], in_=z[at(s, js), :, h_cols].rearrange("j b h -> b j h"))
             if s == 0:
                 load_h_n(0, H_ROUND)
-            gz_rh = loads.tile([P, PACK, ZR], F32)
             for js in pieces(s):
-                nc.sync.dma_start(out=gz_rh[:, js, H_ROUND:], in_=r[at(s, js), :, h_cols].rearrange("j b h -> b j h"))
+                nc.sync.dma_start(out=z_r[:, js, H_ROUND:], in_=r[at(s, js), :, h_cols].rearrange("j b h -> b j h"))
             n_dn = loads.tile([P, PACK, ZR], F32)
             for js in pieces(s):
                 nc.sync.dma_start(out=n_dn[:, js, :H_ROUND], in_=n[at(s, js), :, h_cols].rearrange("j b h -> b j h"))
-            loaded[s] = (g_t, z_t)
-            factors[s] = gz_rh
+            loaded[s] = (g_t, z_t, z_r)
             partners[s] = n_dn
 
         def load_x(c):
@@ -118,15 +118,14 @@ def tile_grucellmodel_pa_v_kernel(tc, input_seq, W_ih, b_ih, gh, r, z, n, grad_o
             nc.sync.dma_start(out=x_rows[:, c, :, :], in_=input_seq[steps].rearrange("j b i -> b j i"))
 
         def square_z_r(s):
-            z_t = loaded[s][1]
-            gz_rh = factors[s]
-            for js in pieces(s):
-                nc.scalar.activation(
-                    out=gz_rh[:, js, :H_ROUND], in_=z_t[:, js, :], func=ACT.Square, bias=minus_half[:]
-                )
-            for js in pieces(s):
-                rh = gz_rh[:, js, H_ROUND:]
-                nc.scalar.activation(out=rh, in_=rh, func=ACT.Square, bias=minus_half[:])
+            z_r = loaded[s][2]
+            factors[s] = ahead.tile([P, PACK, ZR], F32, name="gz_rh")
+            halves = (slice(0, H_ROUND), slice(H_ROUND, ZR)) if s < 4 else (slice(0, ZR),)
+            for cols in halves:
+                for js in pieces(s):
+                    nc.scalar.activation(
+                        out=factors[s][:, js, cols], in_=z_r[:, js, cols], func=ACT.Square, bias=minus_half[:]
+                    )
 
         def square_n(s):
             n_dn = partners[s]
@@ -321,7 +320,7 @@ def tile_grucellmodel_pa_v_kernel(tc, input_seq, W_ih, b_ih, gh, r, z, n, grad_o
             if s + SQUARES_AHEAD < STEPS:
                 square_z_r(s + SQUARES_AHEAD)
             multiply_what_is_ready()
-            empty_psum(nc.scalar.copy, 4)
+            empty_psum(nc.scalar.copy, 3)
             if 0 <= s - 1 < PASSES:
                 group_x(s - 1)
         finish_d_z_d_r(nc.vector, LAST, 0, H_ROUND)

@@ -29,7 +29,7 @@ N_MAX = 512
 LOADS_AHEAD = 5
 SQUARES_AHEAD = 2
 X_LATE = 2
-GPSIMD_COLS = 384
+GPSIMD_COLS = 416
 FIRST_PIECES = (slice(0, 2), slice(2, 4))
 
 FLOPS = 2 * T * B * GATES * H * I
@@ -323,15 +323,16 @@ def tile_grucellmodel_pa_v_kernel(tc, input_seq, W_ih, b_ih, gh, r, z, n, grad_o
             empty_psum(nc.scalar.copy, 3)
             if 0 <= s - 1 < PASSES:
                 group_x(s - 1)
-        finish_d_z_d_r(nc.vector, LAST, 0, H_ROUND)
+        finish_d_z_d_r(nc.vector, LAST, 0, 128)
         quantise_d_n(LAST)
         multiply_what_is_ready()
         empty_psum(nc.scalar.copy, 2)
-        finish_d_z_d_r(nc.vector, LAST, H_ROUND, ZR - M_TILE)
+        finish_d_z_d_r(nc.vector, LAST, 128, 256)
         quantise_d_z_d_r(LAST, 0, 2)
         multiply_what_is_ready()
-        finish_d_z_d_r(nc.vector, LAST, ZR - M_TILE, ZR)
         empty_psum(nc.scalar.copy, 2)
+        finish_d_z_d_r(nc.vector, LAST, 256, 384)
+        finish_d_z_d_r(nc.vector, LAST, 384, 512)
         quantise_d_z_d_r(LAST, 2, 3)
         multiply_what_is_ready()
         quantise_d_z_d_r(LAST, 3, 4)

@@ -29,7 +29,7 @@ N_MAX = 512
 LOADS_AHEAD = 5
 SQUARES_AHEAD = 2
 X_LATE = 2
-GPSIMD_COLS = 416
+GPSIMD_COLS = 376
 FIRST_PIECES = (slice(0, 2), slice(2, 4))
 
 FLOPS = 2 * T * B * GATES * H * I

from contextlib import ExitStack

import concourse.mybir as mybir
from concourse.masks import make_identity

F32 = mybir.dt.float32
BF16 = mybir.dt.bfloat16
U32 = mybir.dt.uint32
U8 = mybir.dt.uint8
E4M3_X4 = mybir.dt.float8_e4m3fn_x4
E5M2_X4 = mybir.dt.float8_e5m2_x4
ALU = mybir.AluOpType
ACT = mybir.ActivationFunctionType

T, B, I, H = 12, 128, 512, 1024
P = 128
PACK = 4
PASSES = T // PACK
GATES = 3
D_R, D_Z, D_N = 0, 1, 2
M_TILE = 128
H_ROUND = 256
ROUNDS = H // H_ROUND
HALVES = H_ROUND // M_TILE
STEPS = ROUNDS * PASSES
LAST = STEPS - 1
ZR = 2 * H_ROUND
N_MAX = 512
LOADS_AHEAD = 5
SQUARES_AHEAD = 2
X_LATE = 2
GPSIMD_COLS = 376
FIRST_PIECES = (slice(0, 2), slice(2, 4))

FLOPS = 2 * T * B * GATES * H * I
BYTES = T * B * I * 2 + B * H * 2 + 3 * T * B * H * 4 + B * T * H * 2 + GATES * H * I * 4


def rows_in_fours(rows):
    return rows.rearrange("p j (c i) -> p c j i", i=4)


def words_in_fours(words):
    return words.rearrange("p (c i) j -> p c j i", i=4)


def tile_grucellmodel_pa_v_kernel(tc, input_seq, W_ih, b_ih, gh, r, z, n, grad_out, out):
    nc = tc.nc
    with ExitStack() as ctx:
        keep = ctx.enter_context(tc.tile_pool(name="keep", bufs=1))
        loads = ctx.enter_context(tc.tile_pool(name="loads", bufs=LOADS_AHEAD + 1))
        ahead = ctx.enter_context(tc.tile_pool(name="ahead", bufs=SQUARES_AHEAD + 2))
        work = ctx.enter_context(tc.tile_pool(name="work", bufs=2))
        grouped = ctx.enter_context(tc.tile_pool(name="grouped", bufs=2))
        packed = ctx.enter_context(tc.tile_pool(name="packed", bufs=X_LATE + 2))
        results = ctx.enter_context(tc.tile_pool(name="results", bufs=GATES * HALVES))
        psum = ctx.enter_context(tc.psum_pool(name="psum", bufs=HALVES))
        psum_operands = ctx.enter_context(tc.psum_pool(name="psum_operands", bufs=1))
        ctx.enter_context(tc.manual_schedule())

        h_n = keep.tile([P, H], BF16)
        minus_half = keep.tile([P, 1], F32)
        warm_up = keep.tile([P, 1], F32)
        identity = keep.tile([P, P], BF16)
        minus_identity = keep.tile([P, P], BF16)
        minus_h_n_psum = psum_operands.tile([P, H], BF16)
        x_rows = keep.tile([P, PASSES, PACK, I], BF16)
        x_codes = keep.tile([P, PASSES, I], U32, align_bytes=64)
        x_scales = keep.tile([P, PASSES, I], U8, align_bytes=64)
        loaded = {}
        factors = {}
        partners = {}
        x_grouped = {}
        g_psum = {}
        g_one_minus_z = {}
        dn_words = {}
        zr_words = {}
        quantised = []
        acc = {}
        occupied = []
        complete = []
        progress = {"x_passes": 0}

        def place(s):
            hq, c = divmod(s, PASSES)
            return slice(c * PACK, (c + 1) * PACK), slice(hq * H_ROUND, (hq + 1) * H_ROUND)

        def pieces(s):
            return FIRST_PIECES if s == 0 else (slice(0, PACK),)

        def at(s, js):
            step0 = (s % PASSES) * PACK
            return slice(step0 + js.start, step0 + js.stop)

        def load_h_n(col0, col1):
            nc.sync.dma_start(out=h_n[:, col0:col1], in_=gh[:, 2 * H + col0 : 2 * H + col1])

        def load(s):
            steps, h_cols = place(s)
            g_t = loads.tile([P, PACK, H_ROUND], BF16)
            nc.sync.dma_start(out=g_t[:], in_=grad_out[:, steps, h_cols])
            z_r = loads.tile([P, PACK, ZR], F32)
            z_t = z_r[:, :, :H_ROUND]
            for js in pieces(s):
                nc.sync.dma_start(out=z_t[:, js, :], in_=z[at(s, js), :, h_cols].rearrange("j b h -> b j h"))
            if s == 0:
                load_h_n(0, H_ROUND)
            for js in pieces(s):
                nc.sync.dma_start(out=z_r[:, js, H_ROUND:], in_=r[at(s, js), :, h_cols].rearrange("j b h -> b j h"))
            n_dn = loads.tile([P, PACK, ZR], F32)
            for js in pieces(s):
                nc.sync.dma_start(out=n_dn[:, js, :H_ROUND], in_=n[at(s, js), :, h_cols].rearrange("j b h -> b j h"))
            loaded[s] = (g_t, z_t, z_r)
            partners[s] = n_dn

        def load_x(c):
            steps = slice(c * PACK, (c + 1) * PACK)
            nc.sync.dma_start(out=x_rows[:, c, :, :], in_=input_seq[steps].rearrange("j b i -> b j i"))

        def square_z_r(s):
            z_r = loaded[s][2]
            factors[s] = ahead.tile([P, PACK, ZR], F32, name="gz_rh")
            halves = (slice(0, H_ROUND), slice(H_ROUND, ZR)) if s < 4 else (slice(0, ZR),)
            for cols in halves:
                for js in pieces(s):
                    nc.scalar.activation(
                        out=factors[s][:, js, cols], in_=z_r[:, js, cols], func=ACT.Square, bias=minus_half[:]
                    )

        def square_n(s):
            n_dn = partners[s]
            for js in pieces(s):
                nc.scalar.activation(out=n_dn[:, js, H_ROUND:], in_=n_dn[:, js, :H_ROUND], func=ACT.Square)

        def copy_into_psum(dst, src, diagonal):
            width = dst.shape[1]
            for col0 in range(0, width, N_MAX):
                cols = slice(col0, min(col0 + N_MAX, width))
                nc.tensor.matmul(
                    out=dst[:, cols],
                    lhsT=diagonal[:],
                    rhs=src[:, cols],
                    start=True,
                    stop=True,
                )

        def copy_g(s):
            g_p = psum_operands.tile([P, PACK * H_ROUND], BF16)
            copy_into_psum(g_p[:], loaded[s][0][:].rearrange("p j h -> p (j h)"), identity)
            g_psum[s] = g_p

        def group_x(c):
            x_words = grouped.tile([P, I, PACK], BF16, align_bytes=64)
            nc.scalar.copy(out=words_in_fours(x_words[:]), in_=rows_in_fours(x_rows[:, c, :, :]))
            x_grouped[c] = x_words

        def multiply_from_psum(s):
            h_cols = place(s)[1]
            z_t = loaded[s][1]
            gz = factors[s][:, :, :H_ROUND]
            rh = factors[s][:, :, H_ROUND:]
            g_rows = g_psum[s][:].rearrange("p (j h) -> p j h", j=PACK)
            gw = work.tile([P, PACK, H_ROUND], F32)
            for js in pieces(s):
                nc.vector.scalar_tensor_tensor(
                    out=gw[:, js, :],
                    in0=z_t[:, js, :],
                    scalar=1.0,
                    in1=g_rows[:, js, :],
                    op0=ALU.subtract,
                    op1=ALU.mult,
                )
            g_one_minus_z[s] = gw
            for js in pieces(s):
                nc.vector.scalar_tensor_tensor(
                    out=gz[:, js, :],
                    in0=gz[:, js, :],
                    scalar=0.25,
                    in1=g_rows[:, js, :],
                    op0=ALU.subtract,
                    op1=ALU.mult,
                )
            if s < LAST:
                copy_g(s + 1)
            for js in pieces(s):
                nc.vector.scalar_tensor_tensor(
                    out=rh[:, js, :],
                    in0=rh[:, js, :],
                    scalar=0.25,
                    in1=minus_h_n_psum[:, h_cols].unsqueeze(1).to_broadcast([P, js.stop - js.start, H_ROUND]),
                    op0=ALU.subtract,
                    op1=ALU.mult,
                )

        def finish_d_n(s):
            d_n = partners[s][:, :, H_ROUND:]
            for js in pieces(s):
                nc.vector.scalar_tensor_tensor(
                    out=d_n[:, js, :],
                    in0=d_n[:, js, :],
                    scalar=1.0,
                    in1=g_one_minus_z[s][:, js, :],
                    op0=ALU.subtract,
                    op1=ALU.mult,
                )
            dn_words[s] = grouped.tile([P, H_ROUND, PACK], BF16, align_bytes=64, name="dn_words")
            nc.scalar.copy(out=words_in_fours(dn_words[s][:]), in_=rows_in_fours(d_n))
            zr_words[s] = grouped.tile([P, ZR, PACK], BF16, align_bytes=64, name="zr_words")

        def finish_d_z_d_r(engine, s, col0, col1):
            engine.tensor_tensor(
                out=words_in_fours(zr_words[s][:, col0:col1, :]),
                in0=rows_in_fours(factors[s][:, :, col0:col1]),
                in1=rows_in_fours(partners[s][:, :, col0:col1]),
                op=ALU.mult,
            )

        def quantise_x(c):
            nc.vector.quantize_mx(
                out=x_codes[:, c, :].bitcast(E4M3_X4),
                scales=x_scales[:, c, :],
                in_=x_grouped[c][:].rearrange("p w j -> p (w j)"),
            )
            progress["x_passes"] = c + 1

        def quantise(s, source, tiles, tag):
            width = len(tiles) * M_TILE
            codes = packed.tile([P, width], U32, align_bytes=64, name="codes", tag="codes_" + tag)
            scales = packed.tile([P, width], U8, align_bytes=64, name="scales", tag="scales_" + tag)
            nc.vector.quantize_mx(
                out=codes[:].bitcast(E5M2_X4),
                scales=scales[:],
                in_=source.rearrange("p w j -> p (w j)"),
            )
            quantised.append((s, tiles, codes, scales))

        def quantise_d_n(s):
            quantise(s, dn_words[s][:], [(D_N, half) for half in range(HALVES)], "n")

        def quantise_d_z_d_r(s, first_tile, last_tile):
            tiles = [(gate, half) for gate in (D_Z, D_R) for half in range(HALVES)]
            quantise(
                s,
                zr_words[s][:, first_tile * M_TILE : last_tile * M_TILE, :],
                tiles[first_tile:last_tile],
                "zr",
            )

        def multiply_what_is_ready():
            for entry in list(quantised):
                s, tiles, codes, scales = entry
                hq, c = divmod(s, PASSES)
                if c >= progress["x_passes"] or (c == 0 and any(t in occupied for t in tiles)):
                    continue
                if c > 0 and any(e[0] < s and e[1][0] == tiles[0] for e in quantised):
                    continue
                quantised.remove(entry)
                for k, (gate, half) in enumerate(tiles):
                    if c == 0:
                        acc[gate, half] = psum.tile([M_TILE, I], F32, name="acc", tag="acc%d" % gate)
                        occupied.append((gate, half))
                    cols = slice(k * M_TILE, (k + 1) * M_TILE)
                    nc.tensor.matmul_mx(
                        out=acc[gate, half][:],
                        lhsT=codes[:, cols].bitcast(E5M2_X4),
                        lhsT_scale=scales[:, cols],
                        rhs=x_codes[:, c, :].bitcast(E4M3_X4),
                        rhs_scale=x_scales[:, c, :],
                        start=(c == 0),
                        stop=(c == PASSES - 1),
                    )
                    if c == PASSES - 1:
                        complete.append((hq, gate, half))

        def empty_psum(copy, count, parts=1):
            for hq, gate, half in complete[:count]:
                row0 = gate * H + hq * H_ROUND + half * M_TILE
                res = results.tile([M_TILE, I], F32)
                for part in range(parts):
                    cols = slice(part * I // parts, (part + 1) * I // parts)
                    copy(out=res[:, cols], in_=acc[gate, half][:, cols])
                    nc.sync.dma_start(out=out[row0 : row0 + M_TILE, cols], in_=res[:, cols])
                occupied.remove((gate, half))
                complete.remove((hq, gate, half))

        nc.vector.memset(minus_half[:], -0.5)
        nc.scalar.activation(out=warm_up[:], in_=minus_half[:], func=ACT.Square)
        make_identity(nc, identity[:])
        nc.vector.tensor_scalar_mul(out=minus_identity[:], in0=identity[:], scalar1=-1.0)
        for s in range(LOADS_AHEAD):
            load(s)
            if s == 1:
                load_h_n(H_ROUND, H)
            if 0 <= s - X_LATE < PASSES:
                load_x(s - X_LATE)
        copy_g(0)
        copy_into_psum(minus_h_n_psum[:, :H_ROUND], h_n[:, :H_ROUND], minus_identity)
        square_z_r(0)
        square_n(0)
        square_z_r(1)

        for s in range(STEPS):
            multiply_from_psum(s)
            if s == 0:
                copy_into_psum(minus_h_n_psum[:, H_ROUND:], h_n[:, H_ROUND:], minus_identity)
            if s >= 1:
                finish_d_z_d_r(nc.vector, s - 1, GPSIMD_COLS, ZR)
                quantise_d_n(s - 1)
            if s + LOADS_AHEAD < STEPS:
                load(s + LOADS_AHEAD)
            if 0 <= s - 1 - X_LATE < PASSES:
                quantise_x(s - 1 - X_LATE)
            finish_d_n(s)
            if s < LAST:
                finish_d_z_d_r(nc.gpsimd, s, 0, GPSIMD_COLS)
            if s >= 1:
                quantise_d_z_d_r(s - 1, 0, 4)
            if s < LAST:
                square_n(s + 1)
            if s + SQUARES_AHEAD < STEPS:
                square_z_r(s + SQUARES_AHEAD)
            multiply_what_is_ready()
            empty_psum(nc.scalar.copy, 3)
            if 0 <= s - 1 < PASSES:
                group_x(s - 1)
        finish_d_z_d_r(nc.vector, LAST, 0, 128)
        quantise_d_n(LAST)
        multiply_what_is_ready()
        empty_psum(nc.scalar.copy, 2)
        finish_d_z_d_r(nc.vector, LAST, 128, 256)
        quantise_d_z_d_r(LAST, 0, 2)
        multiply_what_is_ready()
        empty_psum(nc.scalar.copy, 2)
        finish_d_z_d_r(nc.vector, LAST, 256, 384)
        finish_d_z_d_r(nc.vector, LAST, 384, 512)
        quantise_d_z_d_r(LAST, 2, 3)
        multiply_what_is_ready()
        quantise_d_z_d_r(LAST, 3, 4)
        multiply_what_is_ready()
        empty_psum(nc.vector.tensor_copy, 1, parts=2)
        empty_psum(nc.scalar.copy, 1, parts=2)
